import numpy as np
import ml_dtypes


def mxq(x, axis, fmt="e4m3"):
    dtype, down = {"e4m3": (ml_dtypes.float8_e4m3fn, 7), "e5m2": (ml_dtypes.float8_e5m2, 14)}[fmt]
    v = np.moveaxis(np.asarray(x, np.float32).astype(ml_dtypes.bfloat16).astype(np.float64), axis, -1)
    blocks = v.reshape(v.shape[:-1] + (-1, 32))
    amax = np.abs(blocks).max(-1, keepdims=True)
    byte = np.maximum(np.where(amax > 0, np.frexp(amax)[1] - 1 + 127, 0) - down, 1)
    scale = np.exp2(byte - 127.0)
    codes = (blocks / scale).astype(np.float32).astype(dtype).astype(np.float64)
    return np.moveaxis((codes * scale).reshape(v.shape), -1, axis)


WIDE = False


def mx_kscale(k):
    if not WIDE:
        return np.ones(k)
    levels = np.array([10, -10, 5, -5, 0])
    a = np.random.permutation(np.resize(levels, k // 512 * 4)).reshape(k // 512, 4)
    idx = np.arange(k)
    return np.exp2(a[idx // 512, idx % 128 // 32])


BF16 = ml_dtypes.bfloat16


def bf(x):
    return np.asarray(x, np.float32).astype(BF16)


def f64(x):
    return np.asarray(x).astype(np.float64)


B, C, H, W, O, KH, KW, PH, PW, T, R = 2, 256, 7, 6, 256, 2, 1, 1, 1, 8, 64
HO, WO = H + PH + PH - KH + 1, W + PW + PW - KW + 1
N = B * HO * WO
D = C * KH * KW
R2 = R * KH * KW
K1, K2 = T * R, T * R2


def setup_inputs():
    s, t1, t2 = mx_kscale(D), mx_kscale(K1).reshape(T, R), mx_kscale(K2).reshape(T, R2)
    return {"xw": bf(np.random.standard_normal((N, D)) * s),
            "S1s": bf(np.random.standard_normal((T, D, R)) / np.sqrt(D) / s[None, :, None] * t1[:, None, :]),
            "U1s": bf(np.random.standard_normal((T, R, O)) * T / np.sqrt(K1) / t1[:, :, None]),
            "U2s": bf(np.random.standard_normal((T, R2, D)) / np.sqrt(D) / s[None, None, :] * t2[:, :, None]),
            "S2s": bf(np.random.standard_normal((T, R2, O)) * T / np.sqrt(K2) / t2[:, :, None]),
            "bias": bf(np.random.standard_normal(O) * 0.3)}


def reference(xw, S1s, U1s, U2s, S2s, bias):
    xq = mxq(f64(xw), 1, "e4m3")
    s1 = f64(S1s).transpose(1, 0, 2).reshape(D, K1)
    h1 = xq @ mxq(s1, 0, "e4m3")
    out1 = (mxq(h1, 1, "e4m3") @ mxq(f64(U1s).reshape(K1, O), 0, "e4m3")) / T + f64(bias)
    u2 = f64(U2s).reshape(K2, D)
    h2 = xq @ mxq(u2, 1, "e4m3").T
    out2 = (mxq(h2, 1, "e4m3") @ mxq(f64(S2s).reshape(K2, O), 0, "e4m3")) / T
    out = out1 + out2 + f64(bias)
    return out.reshape(B, HO, WO, O).transpose(0, 3, 1, 2)

@@ -1,0 +1,229 @@
+from contextlib import ExitStack
+
+import concourse.mybir as mybir
+from concourse.masks import make_identity
+
+F32 = mybir.dt.float32
+BF16 = mybir.dt.bfloat16
+U32 = mybir.dt.uint32
+U8 = mybir.dt.uint8
+FP8X4 = mybir.dt.float8_e4m3fn_x4
+
+P = 128
+PACK = 4
+K_PASS = P * PACK
+D = 512
+K1 = 512
+K2 = 1024
+RUNS2 = K2 // K_PASS
+TERMS = 8
+RANK1 = 64
+O = 256
+O_HALVES = O // P
+
+FLOPS = 2 * P * (D * K1 + D * K2 + K1 * O + K2 * O)
+
+
+def cols(i, width):
+    return slice(i * width, (i + 1) * width)
+
+
+def quantise(nc, grouped, codes, scales):
+    nc.vector.quantize_mx(out=codes.bitcast(FP8X4), scales=scales, in_=grouped)
+
+
+def regroup_rows(engine_copy, grouped, raw):
+    engine_copy(
+        out=grouped.rearrange("p (q i t) -> p q t i", i=4, t=PACK),
+        in_=raw.rearrange("p (t q i) -> p q t i", i=4, t=PACK),
+    )
+
+
+def tile_skconv2d_pa_s_kernel(tc, xw, S1s, U1s, U2s, S2s, bias, out):
+    nc = tc.nc
+    with ExitStack() as ctx:
+        consts = ctx.enter_context(tc.tile_pool(name="consts", bufs=1))
+        raw = ctx.enter_context(tc.tile_pool(name="raw", bufs=1))
+        grp = ctx.enter_context(tc.tile_pool(name="grp", bufs=1))
+        mx = ctx.enter_context(tc.tile_pool(name="mx", bufs=1))
+        res = ctx.enter_context(tc.tile_pool(name="res", bufs=2))
+        psum_t = ctx.enter_context(tc.psum_pool(name="psum_t", bufs=3))
+        psum_h = ctx.enter_context(tc.psum_pool(name="psum_h", bufs=3))
+        psum_y = ctx.enter_context(tc.psum_pool(name="psum_y", bufs=2))
+
+        ident_f32 = consts.tile([P, P], F32)
+        make_identity(nc, ident_f32[:])
+        ident_bf16 = consts.tile([P, P], BF16)
+        make_identity(nc, ident_bf16[:])
+        bias_rows = consts.tile([P, P], BF16)
+        nc.vector.memset(bias_rows[:], 0.0)
+
+        x_raw = raw.tile([P, D], BF16)
+        u2_raw = raw.tile([P, RUNS2 * PACK * D], BF16)
+        s1_raw = raw.tile([P, TERMS * PACK * RANK1], BF16)
+        s2_raw = raw.tile([P, RUNS2 * PACK * O], BF16)
+        u1_raw = raw.tile([P, PACK * O], BF16)
+
+        u2_rows = U2s.flatten_outer_dims().rearrange("(g m c) d -> g m (c d)", g=RUNS2, c=PACK)
+        s2_rows = S2s.flatten_outer_dims().rearrange("(g m c) o -> g m (c o)", g=RUNS2, c=PACK)
+        nc.sync.dma_start(out=x_raw[:], in_=xw)
+        nc.sync.dma_start(out=u2_raw[:, cols(0, PACK * D)], in_=u2_rows[0])
+        nc.sync.dma_start(
+            out=s1_raw[:].rearrange("p (t f) -> p t f", t=TERMS),
+            in_=S1s.rearrange("t (p j) r -> p t (j r)", j=PACK),
+        )
+        nc.sync.dma_start(out=u2_raw[:, cols(1, PACK * D)], in_=u2_rows[1])
+        for g in range(RUNS2):
+            nc.sync.dma_start(out=s2_raw[:, cols(g, PACK * O)], in_=s2_rows[g])
+        nc.sync.dma_start(
+            out=u1_raw[:], in_=U1s.flatten_outer_dims().rearrange("(m c) o -> m (c o)", c=PACK)
+        )
+        nc.scalar.dma_start(
+            out=bias_rows[0:O_HALVES, :], in_=bias.rearrange("(h o) -> h o", h=O_HALVES)
+        )
+
+        x_grp = grp.tile([P, P * PACK], BF16, align_bytes=64)
+        u2_grp = grp.tile([P, K2 * PACK], BF16, align_bytes=64)
+        s1_grp = grp.tile([P, K1 * PACK], BF16, align_bytes=64)
+        s2_grp = grp.tile([P, RUNS2 * O * PACK], BF16, align_bytes=64)
+        u1_grp = grp.tile([P, O * PACK], BF16, align_bytes=64)
+        h1_grp = grp.tile([P, P * PACK], BF16, align_bytes=64)
+        h2_grp = grp.tile([P, RUNS2 * P * PACK], BF16, align_bytes=64)
+
+        x_codes = mx.tile([P, P], U32, align_bytes=64)
+        x_scales = mx.tile([P, P], U8, align_bytes=64)
+        u2_codes = mx.tile([P, K2], U32, align_bytes=64)
+        u2_scales = mx.tile([P, K2], U8, align_bytes=64)
+        s1_codes = mx.tile([P, K1], U32, align_bytes=64)
+        s1_scales = mx.tile([P, K1], U8, align_bytes=64)
+        s2_codes = mx.tile([P, RUNS2 * O], U32, align_bytes=64)
+        s2_scales = mx.tile([P, RUNS2 * O], U8, align_bytes=64)
+        u1_codes = mx.tile([P, O], U32, align_bytes=64)
+        u1_scales = mx.tile([P, O], U8, align_bytes=64)
+        h1_codes = mx.tile([P, P], U32, align_bytes=64)
+        h1_scales = mx.tile([P, P], U8, align_bytes=64)
+        h2_codes = mx.tile([P, RUNS2 * P], U32, align_bytes=64)
+        h2_scales = mx.tile([P, RUNS2 * P], U8, align_bytes=64)
+
+        def transpose_rows(bank, rows_bf16):
+            words = rows_bf16.bitcast(F32).rearrange("r (p u) -> r u p", u=2)
+            for u in range(2):
+                nc.tensor.transpose(bank[:, u, :], words[:, u, :], ident_f32[:])
+
+        x_bank = psum_t.tile([P, 2, P], F32, tag="t")
+        transpose_rows(x_bank, x_raw[:])
+        nc.scalar.copy(
+            out=x_grp[:].bitcast(F32).rearrange("p (n u) -> p n u", u=2),
+            in_=x_bank[:].rearrange("p u n -> p n u"),
+        )
+        quantise(nc, x_grp[:], x_codes[:], x_scales[:])
+
+        def stage1(h_bank, w_codes, w_scales, first_piece):
+            for c in range(PACK):
+                piece = cols(first_piece + c, P)
+                nc.tensor.matmul_mx(
+                    out=h_bank[:, c, :],
+                    lhsT=w_codes[:, piece].bitcast(FP8X4),
+                    lhsT_scale=w_scales[:, piece],
+                    rhs=x_codes[:].bitcast(FP8X4),
+                    rhs_scale=x_scales[:],
+                    start=True,
+                    stop=True,
+                )
+
+        def round_and_quantise_h(h_bank, h_grp, h_codes, h_scales):
+            nc.scalar.copy(
+                out=h_grp.rearrange("m (n c) -> m n c", c=PACK),
+                in_=h_bank[:].rearrange("m c n -> m n c"),
+            )
+            quantise(nc, h_grp, h_codes, h_scales)
+
+        def second_sketch_stage1(g):
+            u2_grp_words = u2_grp[:].bitcast(F32).rearrange(
+                "p (k m u) -> p k m u", m=P, u=2
+            )
+            for pair in range(PACK // 2):
+                first = PACK * g + 2 * pair
+                bank = psum_t.tile([P, 2, 2, P], F32, tag="t")
+                for i in range(2):
+                    transpose_rows(bank[:, i], u2_raw[:, cols(first + i, D)])
+                nc.scalar.copy(
+                    out=u2_grp_words[:, first : first + 2],
+                    in_=bank[:].rearrange("p i u m -> p i m u"),
+                )
+            quantise(
+                nc,
+                u2_grp[:, cols(g, K_PASS * PACK)],
+                u2_codes[:, cols(g, K_PASS)],
+                u2_scales[:, cols(g, K_PASS)],
+            )
+            h2_bank = psum_h.tile([P, PACK, P], F32, tag="h")
+            stage1(h2_bank, u2_codes, u2_scales, PACK * g)
+            round_and_quantise_h(
+                h2_bank, h2_grp[:, cols(g, P * PACK)], h2_codes[:, cols(g, P)], h2_scales[:, cols(g, P)]
+            )
+
+        second_sketch_stage1(0)
+
+        s1_by_piece = s1_raw[:].rearrange(
+            "p (t j q c) -> p c t q j", t=TERMS, j=PACK, c=PACK
+        )
+        for c in range(PACK):
+            nc.vector.tensor_copy(
+                out=s1_grp[:, cols(c, P * PACK)].rearrange(
+                    "p (t q j) -> p t q j", t=TERMS, j=PACK
+                ),
+                in_=s1_by_piece[:, c],
+            )
+        quantise(nc, s1_grp[:], s1_codes[:], s1_scales[:])
+        h1_bank = psum_h.tile([P, PACK, P], F32, tag="h")
+        stage1(h1_bank, s1_codes, s1_scales, 0)
+        round_and_quantise_h(h1_bank, h1_grp[:], h1_codes[:], h1_scales[:])
+
+        second_sketch_stage1(1)
+
+        bias_bank = psum_t.tile([P, P], BF16, tag="t")
+        nc.tensor.transpose(bias_bank[:], bias_rows[:], ident_bf16[:])
+        bias_twice = consts.tile([P, O_HALVES], F32)
+        nc.scalar.mul(out=bias_twice[:], in_=bias_bank[:, 0:O_HALVES], mul=2.0)
+
+        for g in range(RUNS2):
+            regroup_rows(
+                nc.vector.tensor_copy, s2_grp[:, cols(g, O * PACK)], s2_raw[:, cols(g, O * PACK)]
+            )
+            quantise(
+                nc, s2_grp[:, cols(g, O * PACK)], s2_codes[:, cols(g, O)], s2_scales[:, cols(g, O)]
+            )
+        regroup_rows(nc.scalar.copy, u1_grp[:], u1_raw[:])
+        quantise(nc, u1_grp[:], u1_codes[:], u1_scales[:])
+
+        out_halves = out.rearrange("b (h o) i j -> h o b (i j)", h=O_HALVES)
+        for h in range(O_HALVES):
+            passes = [
+                (s2_codes[:, cols(g * O_HALVES + h, P)], s2_scales[:, cols(g * O_HALVES + h, P)],
+                 h2_codes[:, cols(g, P)], h2_scales[:, cols(g, P)])
+                for g in range(RUNS2)
+            ]
+            passes.append(
+                (u1_codes[:, cols(h, P)], u1_scales[:, cols(h, P)], h1_codes[:], h1_scales[:])
+            )
+            y_bank = psum_y.tile([P, P], F32, tag="y")
+            for i, (w_codes, w_scales, h_codes, h_scales) in enumerate(passes):
+                nc.tensor.matmul_mx(
+                    out=y_bank[:],
+                    lhsT=w_codes.bitcast(FP8X4),
+                    lhsT_scale=w_scales,
+                    rhs=h_codes.bitcast(FP8X4),
+                    rhs_scale=h_scales,
+                    start=(i == 0),
+                    stop=(i == len(passes) - 1),
+                )
+            y_sb = res.tile([P, P], F32)
+            nc.scalar.activation(
+                out=y_sb[:],
+                in_=y_bank[:],
+                func=mybir.ActivationFunctionType.Identity,
+                bias=bias_twice[:, h : h + 1],
+                scale=1.0 / TERMS,
+            )
+            nc.sync.dma_start(out=out_halves[h], in_=y_sb[:].rearrange("o (b s) -> o b s", b=2))

@@ -20,23 +20,13 @@ TERMS = 8
 RANK1 = 64
 O = 256
 O_HALVES = O // P
+VECTOR_QUARTERS = 3
 
 FLOPS = 2 * P * (D * K1 + D * K2 + K1 * O + K2 * O)
 
 
 def cols(i, width):
     return slice(i * width, (i + 1) * width)
-
-
-def quantise(nc, grouped, codes, scales):
-    nc.vector.quantize_mx(out=codes.bitcast(FP8X4), scales=scales, in_=grouped)
-
-
-def regroup_rows(engine_copy, grouped, raw):
-    engine_copy(
-        out=grouped.rearrange("p (q i t) -> p q t i", i=4, t=PACK),
-        in_=raw.rearrange("p (t q i) -> p q t i", i=4, t=PACK),
-    )
 
 
 def tile_skconv2d_pa_s_kernel(tc, xw, S1s, U1s, U2s, S2s, bias, out):
@@ -50,37 +40,18 @@ def tile_skconv2d_pa_s_kernel(tc, xw, S1s, U1s, U2s, S2s, bias, out):
         psum_t = ctx.enter_context(tc.psum_pool(name="psum_t", bufs=3))
         psum_h = ctx.enter_context(tc.psum_pool(name="psum_h", bufs=3))
         psum_y = ctx.enter_context(tc.psum_pool(name="psum_y", bufs=2))
+        ctx.enter_context(tc.manual_schedule())
 
         ident_f32 = consts.tile([P, P], F32)
-        make_identity(nc, ident_f32[:])
         ident_bf16 = consts.tile([P, P], BF16)
-        make_identity(nc, ident_bf16[:])
         bias_rows = consts.tile([P, P], BF16)
-        nc.vector.memset(bias_rows[:], 0.0)
+        bias_twice = consts.tile([P, O_HALVES], F32)
 
         x_raw = raw.tile([P, D], BF16)
         u2_raw = raw.tile([P, RUNS2 * PACK * D], BF16)
         s1_raw = raw.tile([P, TERMS * PACK * RANK1], BF16)
         s2_raw = raw.tile([P, RUNS2 * PACK * O], BF16)
         u1_raw = raw.tile([P, PACK * O], BF16)
-
-        u2_rows = U2s.flatten_outer_dims().rearrange("(g m c) d -> g m (c d)", g=RUNS2, c=PACK)
-        s2_rows = S2s.flatten_outer_dims().rearrange("(g m c) o -> g m (c o)", g=RUNS2, c=PACK)
-        nc.sync.dma_start(out=x_raw[:], in_=xw)
-        nc.sync.dma_start(out=u2_raw[:, cols(0, PACK * D)], in_=u2_rows[0])
-        nc.sync.dma_start(
-            out=s1_raw[:].rearrange("p (t f) -> p t f", t=TERMS),
-            in_=S1s.rearrange("t (p j) r -> p t (j r)", j=PACK),
-        )
-        nc.sync.dma_start(out=u2_raw[:, cols(1, PACK * D)], in_=u2_rows[1])
-        for g in range(RUNS2):
-            nc.sync.dma_start(out=s2_raw[:, cols(g, PACK * O)], in_=s2_rows[g])
-        nc.sync.dma_start(
-            out=u1_raw[:], in_=U1s.flatten_outer_dims().rearrange("(m c) o -> m (c o)", c=PACK)
-        )
-        nc.scalar.dma_start(
-            out=bias_rows[0:O_HALVES, :], in_=bias.rearrange("(h o) -> h o", h=O_HALVES)
-        )
 
         x_grp = grp.tile([P, P * PACK], BF16, align_bytes=64)
         u2_grp = grp.tile([P, K2 * PACK], BF16, align_bytes=64)
@@ -105,18 +76,20 @@ def tile_skconv2d_pa_s_kernel(tc, xw, S1s, U1s, U2s, S2s, bias, out):
         h2_codes = mx.tile([P, RUNS2 * P], U32, align_bytes=64)
         h2_scales = mx.tile([P, RUNS2 * P], U8, align_bytes=64)
 
+        def quantise(grouped, codes, scales):
+            nc.vector.quantize_mx(out=codes.bitcast(FP8X4), scales=scales, in_=grouped)
+
         def transpose_rows(bank, rows_bf16):
             words = rows_bf16.bitcast(F32).rearrange("r (p u) -> r u p", u=2)
             for u in range(2):
                 nc.tensor.transpose(bank[:, u, :], words[:, u, :], ident_f32[:])
 
-        x_bank = psum_t.tile([P, 2, P], F32, tag="t")
-        transpose_rows(x_bank, x_raw[:])
-        nc.scalar.copy(
-            out=x_grp[:].bitcast(F32).rearrange("p (n u) -> p n u", u=2),
-            in_=x_bank[:].rearrange("p u n -> p n u"),
-        )
-        quantise(nc, x_grp[:], x_codes[:], x_scales[:])
+        def regroup_rows(grouped, rows, width):
+            to = grouped.rearrange("m (q i c) -> m q c i", i=4, c=PACK)
+            frm = rows.rearrange("m (c q i) -> m q c i", i=4, c=PACK)
+            cut = (width // 4) * VECTOR_QUARTERS // 4
+            nc.vector.tensor_copy(out=to[:, 0:cut], in_=frm[:, 0:cut])
+            nc.scalar.copy(out=to[:, cut:], in_=frm[:, cut:])
 
         def stage1(h_bank, w_codes, w_scales, first_piece):
             for c in range(PACK):
@@ -131,99 +104,126 @@ def tile_skconv2d_pa_s_kernel(tc, xw, S1s, U1s, U2s, S2s, bias, out):
                     stop=True,
                 )
 
-        def round_and_quantise_h(h_bank, h_grp, h_codes, h_scales):
+        def round_h(h_bank, h_grp):
             nc.scalar.copy(
                 out=h_grp.rearrange("m (n c) -> m n c", c=PACK),
                 in_=h_bank[:].rearrange("m c n -> m n c"),
             )
-            quantise(nc, h_grp, h_codes, h_scales)
 
-        def second_sketch_stage1(g):
-            u2_grp_words = u2_grp[:].bitcast(F32).rearrange(
-                "p (k m u) -> p k m u", m=P, u=2
-            )
-            for pair in range(PACK // 2):
-                first = PACK * g + 2 * pair
-                bank = psum_t.tile([P, 2, 2, P], F32, tag="t")
-                for i in range(2):
-                    transpose_rows(bank[:, i], u2_raw[:, cols(first + i, D)])
-                nc.scalar.copy(
-                    out=u2_grp_words[:, first : first + 2],
-                    in_=bank[:].rearrange("p i u m -> p i m u"),
+        def stage2(y_banks, w_codes, w_scales, h_codes, h_scales, start, stop):
+            for h in range(O_HALVES):
+                nc.tensor.matmul_mx(
+                    out=y_banks[h][:],
+                    lhsT=w_codes[:, cols(h, P)].bitcast(FP8X4),
+                    lhsT_scale=w_scales[:, cols(h, P)],
+                    rhs=h_codes.bitcast(FP8X4),
+                    rhs_scale=h_scales,
+                    start=start,
+                    stop=stop,
                 )
-            quantise(
-                nc,
-                u2_grp[:, cols(g, K_PASS * PACK)],
-                u2_codes[:, cols(g, K_PASS)],
-                u2_scales[:, cols(g, K_PASS)],
-            )
-            h2_bank = psum_h.tile([P, PACK, P], F32, tag="h")
-            stage1(h2_bank, u2_codes, u2_scales, PACK * g)
-            round_and_quantise_h(
-                h2_bank, h2_grp[:, cols(g, P * PACK)], h2_codes[:, cols(g, P)], h2_scales[:, cols(g, P)]
-            )
 
-        second_sketch_stage1(0)
+        make_identity(nc, ident_f32[:])
+        make_identity(nc, ident_bf16[:])
+        nc.vector.memset(bias_rows[:], 0.0)
 
-        s1_by_piece = s1_raw[:].rearrange(
-            "p (t j q c) -> p c t q j", t=TERMS, j=PACK, c=PACK
+        u2_rows = U2s.flatten_outer_dims().rearrange(
+            "(g m c) d -> m g c d", g=RUNS2, c=PACK
         )
-        for c in range(PACK):
-            nc.vector.tensor_copy(
-                out=s1_grp[:, cols(c, P * PACK)].rearrange(
-                    "p (t q j) -> p t q j", t=TERMS, j=PACK
-                ),
-                in_=s1_by_piece[:, c],
-            )
-        quantise(nc, s1_grp[:], s1_codes[:], s1_scales[:])
-        h1_bank = psum_h.tile([P, PACK, P], F32, tag="h")
-        stage1(h1_bank, s1_codes, s1_scales, 0)
-        round_and_quantise_h(h1_bank, h1_grp[:], h1_codes[:], h1_scales[:])
+        u2_raw_pieces = u2_raw[:].rearrange("m (g c d) -> m g c d", g=RUNS2, c=PACK)
+        s2_rows = S2s.flatten_outer_dims().rearrange("(g m c) o -> g m (c o)", g=RUNS2, c=PACK)
+        nc.sync.dma_start(out=x_raw[:], in_=xw)
+        for g in range(RUNS2):
+            for pair in range(PACK // 2):
+                two = slice(2 * pair, 2 * pair + 2)
+                nc.sync.dma_start(out=u2_raw_pieces[:, g, two, :], in_=u2_rows[:, g, two, :])
+        nc.sync.dma_start(
+            out=s1_raw[:].rearrange("p (t f) -> p t f", t=TERMS),
+            in_=S1s.rearrange("t (p j) r -> p t (j r)", j=PACK),
+        )
+        for g in range(RUNS2):
+            nc.sync.dma_start(out=s2_raw[:, cols(g, PACK * O)], in_=s2_rows[g])
+        nc.sync.dma_start(
+            out=u1_raw[:], in_=U1s.flatten_outer_dims().rearrange("(m c) o -> m (c o)", c=PACK)
+        )
+        nc.scalar.dma_start(
+            out=bias_rows[0:O_HALVES, :], in_=bias.rearrange("(h o) -> h o", h=O_HALVES)
+        )
 
-        second_sketch_stage1(1)
+        x_bank = psum_t.tile([P, 2, P], F32, tag="t")
+        transpose_rows(x_bank, x_raw[:])
+        nc.scalar.copy(
+            out=x_grp[:].bitcast(F32).rearrange("p (n u) -> p n u", u=2),
+            in_=x_bank[:].rearrange("p u n -> p n u"),
+        )
+        quantise(x_grp[:], x_codes[:], x_scales[:])
+
+        u2_grp_words = u2_grp[:].bitcast(F32).rearrange("p (k m u) -> p k m u", m=P, u=2)
+        for pair in range(K2 // P // 2):
+            bank = psum_t.tile([P, 2, 2, P], F32, tag="t")
+            for i in range(2):
+                transpose_rows(bank[:, i], u2_raw[:, cols(2 * pair + i, D)])
+            nc.scalar.copy(
+                out=u2_grp_words[:, 2 * pair : 2 * pair + 2],
+                in_=bank[:].rearrange("p i u m -> p i m u"),
+            )
+            quantise(
+                u2_grp[:, cols(pair, 2 * P * PACK)],
+                u2_codes[:, cols(pair, 2 * P)],
+                u2_scales[:, cols(pair, 2 * P)],
+            )
 
         bias_bank = psum_t.tile([P, P], BF16, tag="t")
         nc.tensor.transpose(bias_bank[:], bias_rows[:], ident_bf16[:])
-        bias_twice = consts.tile([P, O_HALVES], F32)
         nc.scalar.mul(out=bias_twice[:], in_=bias_bank[:, 0:O_HALVES], mul=2.0)
 
+        h2_banks = [psum_h.tile([P, PACK, P], F32, tag="h", name="h2_bank%d" % g) for g in range(RUNS2)]
+        h1_bank = psum_h.tile([P, PACK, P], F32, tag="h")
+
+        stage1(h2_banks[0], u2_codes, u2_scales, 0)
+        round_h(h2_banks[0], h2_grp[:, cols(0, P * PACK)])
+
+        s1_from = s1_raw[:].rearrange("p (t j q c) -> p c t q j", t=TERMS, j=PACK, c=PACK)
+        s1_to = s1_grp[:].rearrange("p (c t q j) -> p c t q j", c=PACK, t=TERMS, j=PACK)
+        nc.vector.tensor_copy(out=s1_to[:, 0:VECTOR_QUARTERS], in_=s1_from[:, 0:VECTOR_QUARTERS])
+        nc.scalar.copy(out=s1_to[:, VECTOR_QUARTERS], in_=s1_from[:, VECTOR_QUARTERS])
+
+        quantise(h2_grp[:, cols(0, P * PACK)], h2_codes[:, cols(0, P)], h2_scales[:, cols(0, P)])
+        quantise(s1_grp[:], s1_codes[:], s1_scales[:])
+
+        stage1(h2_banks[1], u2_codes, u2_scales, PACK)
+        round_h(h2_banks[1], h2_grp[:, cols(1, P * PACK)])
+        quantise(h2_grp[:, cols(1, P * PACK)], h2_codes[:, cols(1, P)], h2_scales[:, cols(1, P)])
+
+        stage1(h1_bank, s1_codes, s1_scales, 0)
+
         for g in range(RUNS2):
-            regroup_rows(
-                nc.vector.tensor_copy, s2_grp[:, cols(g, O * PACK)], s2_raw[:, cols(g, O * PACK)]
+            regroup_rows(s2_grp[:, cols(g, O * PACK)], s2_raw[:, cols(g, O * PACK)], O)
+        quantise(s2_grp[:], s2_codes[:], s2_scales[:])
+
+        round_h(h1_bank, h1_grp[:])
+        quantise(h1_grp[:], h1_codes[:], h1_scales[:])
+
+        regroup_rows(u1_grp[:], u1_raw[:], O)
+        quantise(u1_grp[:], u1_codes[:], u1_scales[:])
+
+        y_banks = [psum_y.tile([P, P], F32, tag="y", name="y_bank%d" % h) for h in range(O_HALVES)]
+        for g in range(RUNS2):
+            stage2(
+                y_banks, s2_codes[:, cols(g, O)], s2_scales[:, cols(g, O)],
+                h2_codes[:, cols(g, P)], h2_scales[:, cols(g, P)], start=(g == 0), stop=False,
             )
-            quantise(
-                nc, s2_grp[:, cols(g, O * PACK)], s2_codes[:, cols(g, O)], s2_scales[:, cols(g, O)]
-            )
-        regroup_rows(nc.scalar.copy, u1_grp[:], u1_raw[:])
-        quantise(nc, u1_grp[:], u1_codes[:], u1_scales[:])
+        stage2(y_banks, u1_codes[:], u1_scales[:], h1_codes[:], h1_scales[:], start=False, stop=True)
 
         out_halves = out.rearrange("b (h o) i j -> h o b (i j)", h=O_HALVES)
-        for h in range(O_HALVES):
-            passes = [
-                (s2_codes[:, cols(g * O_HALVES + h, P)], s2_scales[:, cols(g * O_HALVES + h, P)],
-                 h2_codes[:, cols(g, P)], h2_scales[:, cols(g, P)])
-                for g in range(RUNS2)
-            ]
-            passes.append(
-                (u1_codes[:, cols(h, P)], u1_scales[:, cols(h, P)], h1_codes[:], h1_scales[:])
-            )
-            y_bank = psum_y.tile([P, P], F32, tag="y")
-            for i, (w_codes, w_scales, h_codes, h_scales) in enumerate(passes):
-                nc.tensor.matmul_mx(
-                    out=y_bank[:],
-                    lhsT=w_codes.bitcast(FP8X4),
-                    lhsT_scale=w_scales,
-                    rhs=h_codes.bitcast(FP8X4),
-                    rhs_scale=h_scales,
-                    start=(i == 0),
-                    stop=(i == len(passes) - 1),
-                )
-            y_sb = res.tile([P, P], F32)
-            nc.scalar.activation(
-                out=y_sb[:],
-                in_=y_bank[:],
-                func=mybir.ActivationFunctionType.Identity,
-                bias=bias_twice[:, h : h + 1],
-                scale=1.0 / TERMS,
-            )
-            nc.sync.dma_start(out=out_halves[h], in_=y_sb[:].rearrange("o (b s) -> o b s", b=2))
+        y0 = res.tile([P, P], F32)
+        nc.scalar.activation(
+            out=y0[:], in_=y_banks[0][:], func=mybir.ActivationFunctionType.Identity,
+            bias=bias_twice[:, 0:1], scale=1.0 / TERMS,
+        )
+        nc.sync.dma_start(out=out_halves[0], in_=y0[:].rearrange("o (b s) -> o b s", b=2))
+        y1 = res.tile([P, P], F32)
+        nc.vector.tensor_scalar(
+            out=y1[:], in0=y_banks[1][:], scalar1=1.0 / TERMS, scalar2=bias_twice[:, 1:2],
+            op0=mybir.AluOpType.mult, op1=mybir.AluOpType.add,
+        )
+        nc.sync.dma_start(out=out_halves[1], in_=y1[:].rearrange("o (b s) -> o b s", b=2))

@@ -20,6 +20,7 @@ TERMS = 8
 RANK1 = 64
 O = 256
 O_HALVES = O // P
+PAIRS = K2 // P // 2
 VECTOR_QUARTERS = 3
 
 FLOPS = 2 * P * (D * K1 + D * K2 + K1 * O + K2 * O)
@@ -157,8 +158,12 @@ def tile_skconv2d_pa_s_kernel(tc, xw, S1s, U1s, U2s, S2s, bias, out):
         )
         quantise(x_grp[:], x_codes[:], x_scales[:])
 
+        bias_bank = psum_t.tile([P, P], BF16, tag="t")
+        nc.tensor.transpose(bias_bank[:], bias_rows[:], ident_bf16[:])
+        nc.scalar.mul(out=bias_twice[:], in_=bias_bank[:, 0:O_HALVES], mul=2.0)
+
         u2_grp_words = u2_grp[:].bitcast(F32).rearrange("p (k m u) -> p k m u", m=P, u=2)
-        for pair in range(K2 // P // 2):
+        for pair in range(PAIRS):
             bank = psum_t.tile([P, 2, 2, P], F32, tag="t")
             for i in range(2):
                 transpose_rows(bank[:, i], u2_raw[:, cols(2 * pair + i, D)])
@@ -166,15 +171,25 @@ def tile_skconv2d_pa_s_kernel(tc, xw, S1s, U1s, U2s, S2s, bias, out):
                 out=u2_grp_words[:, 2 * pair : 2 * pair + 2],
                 in_=bank[:].rearrange("p i u m -> p i m u"),
             )
+
+        def quantise_u2(pair):
             quantise(
                 u2_grp[:, cols(pair, 2 * P * PACK)],
                 u2_codes[:, cols(pair, 2 * P)],
                 u2_scales[:, cols(pair, 2 * P)],
             )
 
-        bias_bank = psum_t.tile([P, P], BF16, tag="t")
-        nc.tensor.transpose(bias_bank[:], bias_rows[:], ident_bf16[:])
-        nc.scalar.mul(out=bias_twice[:], in_=bias_bank[:, 0:O_HALVES], mul=2.0)
+        quantise_u2(0)
+        quantise_u2(1)
+
+        s1_from = s1_raw[:].rearrange("p (t j q c) -> p c t q j", t=TERMS, j=PACK, c=PACK)
+        s1_to = s1_grp[:].rearrange("p (c t q j) -> p c t q j", c=PACK, t=TERMS, j=PACK)
+        nc.vector.tensor_copy(out=s1_to[:, 0:VECTOR_QUARTERS], in_=s1_from[:, 0:VECTOR_QUARTERS])
+        nc.scalar.copy(out=s1_to[:, VECTOR_QUARTERS], in_=s1_from[:, VECTOR_QUARTERS])
+
+        quantise_u2(2)
+        quantise_u2(3)
+        quantise(s1_grp[:], s1_codes[:], s1_scales[:])
 
         h2_banks = [psum_h.tile([P, PACK, P], F32, tag="h", name="h2_bank%d" % g) for g in range(RUNS2)]
         h1_bank = psum_h.tile([P, PACK, P], F32, tag="h")
@@ -182,29 +197,21 @@ def tile_skconv2d_pa_s_kernel(tc, xw, S1s, U1s, U2s, S2s, bias, out):
         stage1(h2_banks[0], u2_codes, u2_scales, 0)
         round_h(h2_banks[0], h2_grp[:, cols(0, P * PACK)])
 
-        s1_from = s1_raw[:].rearrange("p (t j q c) -> p c t q j", t=TERMS, j=PACK, c=PACK)
-        s1_to = s1_grp[:].rearrange("p (c t q j) -> p c t q j", c=PACK, t=TERMS, j=PACK)
-        nc.vector.tensor_copy(out=s1_to[:, 0:VECTOR_QUARTERS], in_=s1_from[:, 0:VECTOR_QUARTERS])
-        nc.scalar.copy(out=s1_to[:, VECTOR_QUARTERS], in_=s1_from[:, VECTOR_QUARTERS])
-
-        quantise(h2_grp[:, cols(0, P * PACK)], h2_codes[:, cols(0, P)], h2_scales[:, cols(0, P)])
-        quantise(s1_grp[:], s1_codes[:], s1_scales[:])
+        for g in range(RUNS2):
+            regroup_rows(s2_grp[:, cols(g, O * PACK)], s2_raw[:, cols(g, O * PACK)], O)
 
         stage1(h2_banks[1], u2_codes, u2_scales, PACK)
         round_h(h2_banks[1], h2_grp[:, cols(1, P * PACK)])
-        quantise(h2_grp[:, cols(1, P * PACK)], h2_codes[:, cols(1, P)], h2_scales[:, cols(1, P)])
-
         stage1(h1_bank, s1_codes, s1_scales, 0)
 
-        for g in range(RUNS2):
-            regroup_rows(s2_grp[:, cols(g, O * PACK)], s2_raw[:, cols(g, O * PACK)], O)
+        quantise(h2_grp[:, cols(0, P * PACK)], h2_codes[:, cols(0, P)], h2_scales[:, cols(0, P)])
         quantise(s2_grp[:], s2_codes[:], s2_scales[:])
-
-        round_h(h1_bank, h1_grp[:])
-        quantise(h1_grp[:], h1_codes[:], h1_scales[:])
+        quantise(h2_grp[:, cols(1, P * PACK)], h2_codes[:, cols(1, P)], h2_scales[:, cols(1, P)])
 
         regroup_rows(u1_grp[:], u1_raw[:], O)
+        round_h(h1_bank, h1_grp[:])
         quantise(u1_grp[:], u1_codes[:], u1_scales[:])
+        quantise(h1_grp[:], h1_codes[:], h1_scales[:])
 
         y_banks = [psum_y.tile([P, P], F32, tag="y", name="y_bank%d" % h) for h in range(O_HALVES)]
         for g in range(RUNS2):

@@ -11,15 +11,15 @@ FP8X4 = mybir.dt.float8_e4m3fn_x4
 
 P = 128
 PACK = 4
-K_PASS = P * PACK
+RUN = P * PACK
 D = 512
 K1 = 512
 K2 = 1024
-RUNS2 = K2 // K_PASS
+RUNS2 = K2 // RUN
 TERMS = 8
 RANK1 = 64
 O = 256
-O_HALVES = O // P
+HALVES = O // P
 PAIRS = K2 // P // 2
 VECTOR_QUARTERS = 3
 
@@ -33,61 +33,59 @@ def cols(i, width):
 def tile_skconv2d_pa_s_kernel(tc, xw, S1s, U1s, U2s, S2s, bias, out):
     nc = tc.nc
     with ExitStack() as ctx:
-        consts = ctx.enter_context(tc.tile_pool(name="consts", bufs=1))
-        raw = ctx.enter_context(tc.tile_pool(name="raw", bufs=1))
-        grp = ctx.enter_context(tc.tile_pool(name="grp", bufs=1))
-        mx = ctx.enter_context(tc.tile_pool(name="mx", bufs=1))
-        res = ctx.enter_context(tc.tile_pool(name="res", bufs=2))
+        sbuf = ctx.enter_context(tc.tile_pool(name="sbuf", bufs=1))
         psum_t = ctx.enter_context(tc.psum_pool(name="psum_t", bufs=3))
-        psum_h = ctx.enter_context(tc.psum_pool(name="psum_h", bufs=3))
-        psum_y = ctx.enter_context(tc.psum_pool(name="psum_y", bufs=2))
+        psum_h = ctx.enter_context(tc.psum_pool(name="psum_h", bufs=RUNS2 + 1))
+        psum_y = ctx.enter_context(tc.psum_pool(name="psum_y", bufs=HALVES))
         ctx.enter_context(tc.manual_schedule())
 
-        ident_f32 = consts.tile([P, P], F32)
-        ident_bf16 = consts.tile([P, P], BF16)
-        bias_rows = consts.tile([P, P], BF16)
-        bias_twice = consts.tile([P, O_HALVES], F32)
+        ident_f32 = sbuf.tile([P, P], F32)
+        ident_bf16 = sbuf.tile([P, P], BF16)
+        bias_rows = sbuf.tile([P, P], BF16)
+        bias_twice = sbuf.tile([P, HALVES], F32)
 
-        x_raw = raw.tile([P, D], BF16)
-        u2_raw = raw.tile([P, RUNS2 * PACK * D], BF16)
-        s1_raw = raw.tile([P, TERMS * PACK * RANK1], BF16)
-        s2_raw = raw.tile([P, RUNS2 * PACK * O], BF16)
-        u1_raw = raw.tile([P, PACK * O], BF16)
+        x_raw = sbuf.tile([P, D], BF16)
+        u2_raw = sbuf.tile([P, RUNS2 * PACK * D], BF16)
+        s1_raw = sbuf.tile([P, TERMS * PACK * RANK1], BF16)
+        s2_raw = sbuf.tile([P, RUNS2 * PACK * O], BF16)
+        u1_raw = sbuf.tile([P, PACK * O], BF16)
 
-        x_grp = grp.tile([P, P * PACK], BF16, align_bytes=64)
-        u2_grp = grp.tile([P, K2 * PACK], BF16, align_bytes=64)
-        s1_grp = grp.tile([P, K1 * PACK], BF16, align_bytes=64)
-        s2_grp = grp.tile([P, RUNS2 * O * PACK], BF16, align_bytes=64)
-        u1_grp = grp.tile([P, O * PACK], BF16, align_bytes=64)
-        h1_grp = grp.tile([P, P * PACK], BF16, align_bytes=64)
-        h2_grp = grp.tile([P, RUNS2 * P * PACK], BF16, align_bytes=64)
+        x_grp = sbuf.tile([P, P * PACK], BF16, align_bytes=64)
+        u2_grp = sbuf.tile([P, K2 * PACK], BF16, align_bytes=64)
+        s1_grp = sbuf.tile([P, K1 * PACK], BF16, align_bytes=64)
+        s2_grp = sbuf.tile([P, RUNS2 * O * PACK], BF16, align_bytes=64)
+        u1_grp = sbuf.tile([P, O * PACK], BF16, align_bytes=64)
+        h1_grp = sbuf.tile([P, P * PACK], BF16, align_bytes=64)
+        h2_grp = sbuf.tile([P, RUNS2 * P * PACK], BF16, align_bytes=64)
 
-        x_codes = mx.tile([P, P], U32, align_bytes=64)
-        x_scales = mx.tile([P, P], U8, align_bytes=64)
-        u2_codes = mx.tile([P, K2], U32, align_bytes=64)
-        u2_scales = mx.tile([P, K2], U8, align_bytes=64)
-        s1_codes = mx.tile([P, K1], U32, align_bytes=64)
-        s1_scales = mx.tile([P, K1], U8, align_bytes=64)
-        s2_codes = mx.tile([P, RUNS2 * O], U32, align_bytes=64)
-        s2_scales = mx.tile([P, RUNS2 * O], U8, align_bytes=64)
-        u1_codes = mx.tile([P, O], U32, align_bytes=64)
-        u1_scales = mx.tile([P, O], U8, align_bytes=64)
-        h1_codes = mx.tile([P, P], U32, align_bytes=64)
-        h1_scales = mx.tile([P, P], U8, align_bytes=64)
-        h2_codes = mx.tile([P, RUNS2 * P], U32, align_bytes=64)
-        h2_scales = mx.tile([P, RUNS2 * P], U8, align_bytes=64)
+        x_codes = sbuf.tile([P, P], U32, align_bytes=64)
+        x_scales = sbuf.tile([P, P], U8, align_bytes=64)
+        u2_codes = sbuf.tile([P, K2], U32, align_bytes=64)
+        u2_scales = sbuf.tile([P, K2], U8, align_bytes=64)
+        s1_codes = sbuf.tile([P, K1], U32, align_bytes=64)
+        s1_scales = sbuf.tile([P, K1], U8, align_bytes=64)
+        s2_codes = sbuf.tile([P, RUNS2 * O], U32, align_bytes=64)
+        s2_scales = sbuf.tile([P, RUNS2 * O], U8, align_bytes=64)
+        u1_codes = sbuf.tile([P, O], U32, align_bytes=64)
+        u1_scales = sbuf.tile([P, O], U8, align_bytes=64)
+        h1_codes = sbuf.tile([P, P], U32, align_bytes=64)
+        h1_scales = sbuf.tile([P, P], U8, align_bytes=64)
+        h2_codes = sbuf.tile([P, RUNS2 * P], U32, align_bytes=64)
+        h2_scales = sbuf.tile([P, RUNS2 * P], U8, align_bytes=64)
+
+        y_sb = [sbuf.tile([P, P], F32, name="y_sb%d" % half) for half in range(HALVES)]
 
         def quantise(grouped, codes, scales):
             nc.vector.quantize_mx(out=codes.bitcast(FP8X4), scales=scales, in_=grouped)
 
-        def transpose_rows(bank, rows_bf16):
-            words = rows_bf16.bitcast(F32).rearrange("r (p u) -> r u p", u=2)
+        def transpose_rows(bank, rows):
+            words = rows.bitcast(F32).rearrange("row (p u) -> row u p", u=2)
             for u in range(2):
                 nc.tensor.transpose(bank[:, u, :], words[:, u, :], ident_f32[:])
 
         def regroup_rows(grouped, rows, width):
-            to = grouped.rearrange("m (q i c) -> m q c i", i=4, c=PACK)
-            frm = rows.rearrange("m (c q i) -> m q c i", i=4, c=PACK)
+            to = grouped.rearrange("m (q v c) -> m q c v", v=4, c=PACK)
+            frm = rows.rearrange("m (c q v) -> m q c v", v=4, c=PACK)
             cut = (width // 4) * VECTOR_QUARTERS // 4
             nc.vector.tensor_copy(out=to[:, 0:cut], in_=frm[:, 0:cut])
             nc.scalar.copy(out=to[:, cut:], in_=frm[:, cut:])
@@ -111,12 +109,12 @@ def tile_skconv2d_pa_s_kernel(tc, xw, S1s, U1s, U2s, S2s, bias, out):
                 in_=h_bank[:].rearrange("m c n -> m n c"),
             )
 
-        def stage2(y_banks, w_codes, w_scales, h_codes, h_scales, start, stop):
-            for h in range(O_HALVES):
+        def stage2(w_codes, w_scales, h_codes, h_scales, start, stop):
+            for half in range(HALVES):
                 nc.tensor.matmul_mx(
-                    out=y_banks[h][:],
-                    lhsT=w_codes[:, cols(h, P)].bitcast(FP8X4),
-                    lhsT_scale=w_scales[:, cols(h, P)],
+                    out=y_banks[half][:],
+                    lhsT=w_codes[:, cols(half, P)].bitcast(FP8X4),
+                    lhsT_scale=w_scales[:, cols(half, P)],
                     rhs=h_codes.bitcast(FP8X4),
                     rhs_scale=h_scales,
                     start=start,
@@ -126,16 +124,17 @@ def tile_skconv2d_pa_s_kernel(tc, xw, S1s, U1s, U2s, S2s, bias, out):
         make_identity(nc, ident_f32[:])
         make_identity(nc, ident_bf16[:])
         nc.vector.memset(bias_rows[:], 0.0)
-
-        u2_rows = U2s.flatten_outer_dims().rearrange(
-            "(g m c) d -> m g c d", g=RUNS2, c=PACK
+        nc.scalar.dma_start(
+            out=bias_rows[0:HALVES, :], in_=bias.rearrange("(half o) -> half o", half=HALVES)
         )
+
+        u2_rows = U2s.flatten_outer_dims().rearrange("(g m c) d -> m g c d", g=RUNS2, c=PACK)
         u2_raw_pieces = u2_raw[:].rearrange("m (g c d) -> m g c d", g=RUNS2, c=PACK)
         s2_rows = S2s.flatten_outer_dims().rearrange("(g m c) o -> g m (c o)", g=RUNS2, c=PACK)
         nc.sync.dma_start(out=x_raw[:], in_=xw)
         for g in range(RUNS2):
-            for pair in range(PACK // 2):
-                two = slice(2 * pair, 2 * pair + 2)
+            for first_c in range(0, PACK, 2):
+                two = slice(first_c, first_c + 2)
                 nc.sync.dma_start(out=u2_raw_pieces[:, g, two, :], in_=u2_rows[:, g, two, :])
         nc.sync.dma_start(
             out=s1_raw[:].rearrange("p (t f) -> p t f", t=TERMS),
@@ -145,9 +144,6 @@ def tile_skconv2d_pa_s_kernel(tc, xw, S1s, U1s, U2s, S2s, bias, out):
             nc.sync.dma_start(out=s2_raw[:, cols(g, PACK * O)], in_=s2_rows[g])
         nc.sync.dma_start(
             out=u1_raw[:], in_=U1s.flatten_outer_dims().rearrange("(m c) o -> m (c o)", c=PACK)
-        )
-        nc.scalar.dma_start(
-            out=bias_rows[0:O_HALVES, :], in_=bias.rearrange("(h o) -> h o", h=O_HALVES)
         )
 
         x_bank = psum_t.tile([P, 2, P], F32, tag="t")
@@ -160,9 +156,9 @@ def tile_skconv2d_pa_s_kernel(tc, xw, S1s, U1s, U2s, S2s, bias, out):
 
         bias_bank = psum_t.tile([P, P], BF16, tag="t")
         nc.tensor.transpose(bias_bank[:], bias_rows[:], ident_bf16[:])
-        nc.scalar.mul(out=bias_twice[:], in_=bias_bank[:, 0:O_HALVES], mul=2.0)
+        nc.scalar.mul(out=bias_twice[:], in_=bias_bank[:, 0:HALVES], mul=2.0)
 
-        u2_grp_words = u2_grp[:].bitcast(F32).rearrange("p (k m u) -> p k m u", m=P, u=2)
+        u2_grp_words = u2_grp[:].bitcast(F32).rearrange("p (piece m u) -> p piece m u", m=P, u=2)
         for pair in range(PAIRS):
             bank = psum_t.tile([P, 2, 2, P], F32, tag="t")
             for i in range(2):
@@ -180,57 +176,67 @@ def tile_skconv2d_pa_s_kernel(tc, xw, S1s, U1s, U2s, S2s, bias, out):
             )
 
         quantise_u2(0)
-        quantise_u2(1)
-
-        s1_from = s1_raw[:].rearrange("p (t j q c) -> p c t q j", t=TERMS, j=PACK, c=PACK)
-        s1_to = s1_grp[:].rearrange("p (c t q j) -> p c t q j", c=PACK, t=TERMS, j=PACK)
-        nc.vector.tensor_copy(out=s1_to[:, 0:VECTOR_QUARTERS], in_=s1_from[:, 0:VECTOR_QUARTERS])
-        nc.scalar.copy(out=s1_to[:, VECTOR_QUARTERS], in_=s1_from[:, VECTOR_QUARTERS])
-
-        quantise_u2(2)
-        quantise_u2(3)
+        nc.vector.tensor_copy(
+            out=s1_grp[:].rearrange("p (c t q j) -> p c t q j", c=PACK, t=TERMS, j=PACK),
+            in_=s1_raw[:].rearrange("p (t j q c) -> p c t q j", t=TERMS, j=PACK, c=PACK),
+        )
+        for pair in range(1, PAIRS):
+            quantise_u2(pair)
         quantise(s1_grp[:], s1_codes[:], s1_scales[:])
 
-        h2_banks = [psum_h.tile([P, PACK, P], F32, tag="h", name="h2_bank%d" % g) for g in range(RUNS2)]
+        h2_banks = [
+            psum_h.tile([P, PACK, P], F32, tag="h", name="h2_bank%d" % g) for g in range(RUNS2)
+        ]
         h1_bank = psum_h.tile([P, PACK, P], F32, tag="h")
-
-        stage1(h2_banks[0], u2_codes, u2_scales, 0)
-        round_h(h2_banks[0], h2_grp[:, cols(0, P * PACK)])
+        for g in range(RUNS2):
+            stage1(h2_banks[g], u2_codes, u2_scales, PACK * g)
+        stage1(h1_bank, s1_codes, s1_scales, 0)
 
         for g in range(RUNS2):
             regroup_rows(s2_grp[:, cols(g, O * PACK)], s2_raw[:, cols(g, O * PACK)], O)
-
-        stage1(h2_banks[1], u2_codes, u2_scales, PACK)
-        round_h(h2_banks[1], h2_grp[:, cols(1, P * PACK)])
-        stage1(h1_bank, s1_codes, s1_scales, 0)
-
-        quantise(h2_grp[:, cols(0, P * PACK)], h2_codes[:, cols(0, P)], h2_scales[:, cols(0, P)])
-        quantise(s2_grp[:], s2_codes[:], s2_scales[:])
-        quantise(h2_grp[:, cols(1, P * PACK)], h2_codes[:, cols(1, P)], h2_scales[:, cols(1, P)])
-
         regroup_rows(u1_grp[:], u1_raw[:], O)
+
+        for g in range(RUNS2):
+            round_h(h2_banks[g], h2_grp[:, cols(g, P * PACK)])
         round_h(h1_bank, h1_grp[:])
+
+        quantise(s2_grp[:], s2_codes[:], s2_scales[:])
+        for g in range(RUNS2):
+            quantise(h2_grp[:, cols(g, P * PACK)], h2_codes[:, cols(g, P)], h2_scales[:, cols(g, P)])
         quantise(u1_grp[:], u1_codes[:], u1_scales[:])
         quantise(h1_grp[:], h1_codes[:], h1_scales[:])
 
-        y_banks = [psum_y.tile([P, P], F32, tag="y", name="y_bank%d" % h) for h in range(O_HALVES)]
+        y_banks = [
+            psum_y.tile([P, P], F32, tag="y", name="y_bank%d" % half) for half in range(HALVES)
+        ]
         for g in range(RUNS2):
             stage2(
-                y_banks, s2_codes[:, cols(g, O)], s2_scales[:, cols(g, O)],
-                h2_codes[:, cols(g, P)], h2_scales[:, cols(g, P)], start=(g == 0), stop=False,
+                s2_codes[:, cols(g, O)],
+                s2_scales[:, cols(g, O)],
+                h2_codes[:, cols(g, P)],
+                h2_scales[:, cols(g, P)],
+                start=(g == 0),
+                stop=False,
             )
-        stage2(y_banks, u1_codes[:], u1_scales[:], h1_codes[:], h1_scales[:], start=False, stop=True)
+        stage2(u1_codes[:], u1_scales[:], h1_codes[:], h1_scales[:], start=False, stop=True)
 
-        out_halves = out.rearrange("b (h o) i j -> h o b (i j)", h=O_HALVES)
-        y0 = res.tile([P, P], F32)
         nc.scalar.activation(
-            out=y0[:], in_=y_banks[0][:], func=mybir.ActivationFunctionType.Identity,
-            bias=bias_twice[:, 0:1], scale=1.0 / TERMS,
+            out=y_sb[0][:],
+            in_=y_banks[0][:],
+            func=mybir.ActivationFunctionType.Identity,
+            bias=bias_twice[:, 0:1],
+            scale=1.0 / TERMS,
         )
-        nc.sync.dma_start(out=out_halves[0], in_=y0[:].rearrange("o (b s) -> o b s", b=2))
-        y1 = res.tile([P, P], F32)
         nc.vector.tensor_scalar(
-            out=y1[:], in0=y_banks[1][:], scalar1=1.0 / TERMS, scalar2=bias_twice[:, 1:2],
-            op0=mybir.AluOpType.mult, op1=mybir.AluOpType.add,
+            out=y_sb[1][:],
+            in0=y_banks[1][:],
+            scalar1=1.0 / TERMS,
+            scalar2=bias_twice[:, 1:2],
+            op0=mybir.AluOpType.mult,
+            op1=mybir.AluOpType.add,
         )
-        nc.sync.dma_start(out=out_halves[1], in_=y1[:].rearrange("o (b s) -> o b s", b=2))
+        out_halves = out.rearrange("b (half o) row col -> half o b (row col)", half=HALVES)
+        for half in range(HALVES):
+            nc.sync.dma_start(
+                out=out_halves[half], in_=y_sb[half][:].rearrange("o (b s) -> o b s", b=2)
+            )

@@ -175,12 +175,13 @@ def tile_skconv2d_pa_s_kernel(tc, xw, S1s, U1s, U2s, S2s, bias, out):
                 u2_scales[:, cols(pair, 2 * P)],
             )
 
-        quantise_u2(0)
-        nc.vector.tensor_copy(
-            out=s1_grp[:].rearrange("p (c t q j) -> p c t q j", c=PACK, t=TERMS, j=PACK),
-            in_=s1_raw[:].rearrange("p (t j q c) -> p c t q j", t=TERMS, j=PACK, c=PACK),
-        )
-        for pair in range(1, PAIRS):
+        s1_to = s1_grp[:].rearrange("p (c t q j) -> p c t q j", c=PACK, t=TERMS, j=PACK)
+        s1_from = s1_raw[:].rearrange("p (t j q c) -> p c t q j", t=TERMS, j=PACK, c=PACK)
+        for pair in range(PAIRS // 2):
+            quantise_u2(pair)
+        nc.vector.tensor_copy(out=s1_to[:, 0:VECTOR_QUARTERS], in_=s1_from[:, 0:VECTOR_QUARTERS])
+        nc.scalar.copy(out=s1_to[:, VECTOR_QUARTERS], in_=s1_from[:, VECTOR_QUARTERS])
+        for pair in range(PAIRS // 2, PAIRS):
             quantise_u2(pair)
         quantise(s1_grp[:], s1_codes[:], s1_scales[:])
 

@@ -17,17 +17,22 @@ K1 = 512
 K2 = 1024
 RUNS2 = K2 // RUN
 TERMS = 8
+HALF_TERMS = TERMS // 2
 RANK1 = 64
 O = 256
 HALVES = O // P
-PAIRS = K2 // P // 2
+BATCH = 2
+WORDS = 2
+PAIR = 2
+PAIRS = K2 // P // PAIR
+GROUP = 4
 VECTOR_QUARTERS = 3
 
 FLOPS = 2 * P * (D * K1 + D * K2 + K1 * O + K2 * O)
 
 
-def cols(i, width):
-    return slice(i * width, (i + 1) * width)
+def cols(index, width):
+    return slice(index * width, (index + 1) * width)
 
 
 def tile_skconv2d_pa_s_kernel(tc, xw, S1s, U1s, U2s, S2s, bias, out):
@@ -79,14 +84,14 @@ def tile_skconv2d_pa_s_kernel(tc, xw, S1s, U1s, U2s, S2s, bias, out):
             nc.vector.quantize_mx(out=codes.bitcast(FP8X4), scales=scales, in_=grouped)
 
         def transpose_rows(bank, rows):
-            words = rows.bitcast(F32).rearrange("row (p u) -> row u p", u=2)
-            for u in range(2):
+            words = rows.bitcast(F32).rearrange("row (p u) -> row u p", u=WORDS)
+            for u in range(WORDS):
                 nc.tensor.transpose(bank[:, u, :], words[:, u, :], ident_f32[:])
 
         def regroup_rows(grouped, rows, width):
-            to = grouped.rearrange("m (q v c) -> m q c v", v=4, c=PACK)
-            frm = rows.rearrange("m (c q v) -> m q c v", v=4, c=PACK)
-            cut = (width // 4) * VECTOR_QUARTERS // 4
+            to = grouped.rearrange("m (wg v c) -> m wg c v", v=GROUP, c=PACK)
+            frm = rows.rearrange("m (c wg v) -> m wg c v", v=GROUP, c=PACK)
+            cut = (width // GROUP) * VECTOR_QUARTERS // 4
             nc.vector.tensor_copy(out=to[:, 0:cut], in_=frm[:, 0:cut])
             nc.scalar.copy(out=to[:, cut:], in_=frm[:, cut:])
 
@@ -130,26 +135,26 @@ def tile_skconv2d_pa_s_kernel(tc, xw, S1s, U1s, U2s, S2s, bias, out):
 
         u2_rows = U2s.flatten_outer_dims().rearrange("(g m c) d -> m g c d", g=RUNS2, c=PACK)
         u2_raw_pieces = u2_raw[:].rearrange("m (g c d) -> m g c d", g=RUNS2, c=PACK)
+        s1_rows = S1s.rearrange("t (p a) r -> p t (a r)", a=PACK)
+        s1_raw_terms = s1_raw[:].rearrange("p (t ar) -> p t ar", t=TERMS)
         s2_rows = S2s.flatten_outer_dims().rearrange("(g m c) o -> g m (c o)", g=RUNS2, c=PACK)
         nc.sync.dma_start(out=x_raw[:], in_=xw)
         for g in range(RUNS2):
-            for first_c in range(0, PACK, 2):
-                two = slice(first_c, first_c + 2)
+            for first_c in range(0, PACK, PAIR):
+                two = slice(first_c, first_c + PAIR)
                 nc.sync.dma_start(out=u2_raw_pieces[:, g, two, :], in_=u2_rows[:, g, two, :])
-        nc.sync.dma_start(
-            out=s1_raw[:].rearrange("p (t f) -> p t f", t=TERMS),
-            in_=S1s.rearrange("t (p j) r -> p t (j r)", j=PACK),
-        )
+            four = cols(g, HALF_TERMS)
+            nc.sync.dma_start(out=s1_raw_terms[:, four, :], in_=s1_rows[:, four, :])
         for g in range(RUNS2):
             nc.sync.dma_start(out=s2_raw[:, cols(g, PACK * O)], in_=s2_rows[g])
         nc.sync.dma_start(
             out=u1_raw[:], in_=U1s.flatten_outer_dims().rearrange("(m c) o -> m (c o)", c=PACK)
         )
 
-        x_bank = psum_t.tile([P, 2, P], F32, tag="t")
+        x_bank = psum_t.tile([P, WORDS, P], F32, tag="t")
         transpose_rows(x_bank, x_raw[:])
         nc.scalar.copy(
-            out=x_grp[:].bitcast(F32).rearrange("p (n u) -> p n u", u=2),
+            out=x_grp[:].bitcast(F32).rearrange("p (n u) -> p n u", u=WORDS),
             in_=x_bank[:].rearrange("p u n -> p n u"),
         )
         quantise(x_grp[:], x_codes[:], x_scales[:])
@@ -158,68 +163,86 @@ def tile_skconv2d_pa_s_kernel(tc, xw, S1s, U1s, U2s, S2s, bias, out):
         nc.tensor.transpose(bias_bank[:], bias_rows[:], ident_bf16[:])
         nc.scalar.mul(out=bias_twice[:], in_=bias_bank[:, 0:HALVES], mul=2.0)
 
-        u2_grp_words = u2_grp[:].bitcast(F32).rearrange("p (piece m u) -> p piece m u", m=P, u=2)
+        u2_grp_words = u2_grp[:].bitcast(F32).rearrange(
+            "p (piece m u) -> p piece m u", m=P, u=WORDS
+        )
         for pair in range(PAIRS):
-            bank = psum_t.tile([P, 2, 2, P], F32, tag="t")
-            for i in range(2):
-                transpose_rows(bank[:, i], u2_raw[:, cols(2 * pair + i, D)])
+            bank = psum_t.tile([P, PAIR, WORDS, P], F32, tag="t")
+            for which in range(PAIR):
+                transpose_rows(bank[:, which], u2_raw[:, cols(PAIR * pair + which, D)])
             nc.scalar.copy(
-                out=u2_grp_words[:, 2 * pair : 2 * pair + 2],
-                in_=bank[:].rearrange("p i u m -> p i m u"),
+                out=u2_grp_words[:, PAIR * pair : PAIR * (pair + 1)],
+                in_=bank[:].rearrange("p which u m -> p which m u"),
             )
 
         def quantise_u2(pair):
             quantise(
-                u2_grp[:, cols(pair, 2 * P * PACK)],
-                u2_codes[:, cols(pair, 2 * P)],
-                u2_scales[:, cols(pair, 2 * P)],
+                u2_grp[:, cols(pair, PAIR * P * PACK)],
+                u2_codes[:, cols(pair, PAIR * P)],
+                u2_scales[:, cols(pair, PAIR * P)],
             )
 
-        s1_to = s1_grp[:].rearrange("p (c t q j) -> p c t q j", c=PACK, t=TERMS, j=PACK)
-        s1_from = s1_raw[:].rearrange("p (t j q c) -> p c t q j", t=TERMS, j=PACK, c=PACK)
-        for pair in range(PAIRS // 2):
-            quantise_u2(pair)
-        nc.vector.tensor_copy(out=s1_to[:, 0:VECTOR_QUARTERS], in_=s1_from[:, 0:VECTOR_QUARTERS])
-        nc.scalar.copy(out=s1_to[:, VECTOR_QUARTERS], in_=s1_from[:, VECTOR_QUARTERS])
-        for pair in range(PAIRS // 2, PAIRS):
-            quantise_u2(pair)
+        def regroup_s1(part):
+            four = cols(part, HALF_TERMS)
+            nc.vector.tensor_copy(
+                out=s1_grp[:].rearrange("p (c t q a) -> p c t q a", c=PACK, t=TERMS, a=PACK)[
+                    :, :, four
+                ],
+                in_=s1_raw[:].rearrange("p (t a q c) -> p c t q a", t=TERMS, a=PACK, c=PACK)[
+                    :, :, four
+                ],
+            )
+
+        regroup_s1(0)
+        quantise_u2(0)
+        regroup_s1(1)
+        quantise_u2(1)
+        quantise_u2(2)
         quantise(s1_grp[:], s1_codes[:], s1_scales[:])
+        quantise_u2(3)
 
         h2_banks = [
             psum_h.tile([P, PACK, P], F32, tag="h", name="h2_bank%d" % g) for g in range(RUNS2)
         ]
         h1_bank = psum_h.tile([P, PACK, P], F32, tag="h")
-        for g in range(RUNS2):
-            stage1(h2_banks[g], u2_codes, u2_scales, PACK * g)
+        stage1(h2_banks[0], u2_codes, u2_scales, 0)
         stage1(h1_bank, s1_codes, s1_scales, 0)
+        stage1(h2_banks[1], u2_codes, u2_scales, PACK)
 
         for g in range(RUNS2):
             regroup_rows(s2_grp[:, cols(g, O * PACK)], s2_raw[:, cols(g, O * PACK)], O)
         regroup_rows(u1_grp[:], u1_raw[:], O)
 
-        for g in range(RUNS2):
-            round_h(h2_banks[g], h2_grp[:, cols(g, P * PACK)])
+        def quantise_h2(g):
+            quantise(h2_grp[:, cols(g, P * PACK)], h2_codes[:, cols(g, P)], h2_scales[:, cols(g, P)])
+
+        round_h(h2_banks[0], h2_grp[:, cols(0, P * PACK)])
         round_h(h1_bank, h1_grp[:])
+        round_h(h2_banks[1], h2_grp[:, cols(1, P * PACK)])
 
         quantise(s2_grp[:], s2_codes[:], s2_scales[:])
-        for g in range(RUNS2):
-            quantise(h2_grp[:, cols(g, P * PACK)], h2_codes[:, cols(g, P)], h2_scales[:, cols(g, P)])
+        quantise_h2(0)
         quantise(u1_grp[:], u1_codes[:], u1_scales[:])
         quantise(h1_grp[:], h1_codes[:], h1_scales[:])
+        quantise_h2(1)
 
         y_banks = [
             psum_y.tile([P, P], F32, tag="y", name="y_bank%d" % half) for half in range(HALVES)
         ]
-        for g in range(RUNS2):
+
+        def stage2_of_h2(g, start, stop):
             stage2(
                 s2_codes[:, cols(g, O)],
                 s2_scales[:, cols(g, O)],
                 h2_codes[:, cols(g, P)],
                 h2_scales[:, cols(g, P)],
-                start=(g == 0),
-                stop=False,
+                start=start,
+                stop=stop,
             )
-        stage2(u1_codes[:], u1_scales[:], h1_codes[:], h1_scales[:], start=False, stop=True)
+
+        stage2_of_h2(0, start=True, stop=False)
+        stage2(u1_codes[:], u1_scales[:], h1_codes[:], h1_scales[:], start=False, stop=False)
+        stage2_of_h2(1, start=False, stop=True)
 
         nc.scalar.activation(
             out=y_sb[0][:],
@@ -236,8 +259,8 @@ def tile_skconv2d_pa_s_kernel(tc, xw, S1s, U1s, U2s, S2s, bias, out):
             op0=mybir.AluOpType.mult,
             op1=mybir.AluOpType.add,
         )
-        out_halves = out.rearrange("b (half o) row col -> half o b (row col)", half=HALVES)
+        out_halves = out.rearrange("b (half o) i j -> half o b (i j)", half=HALVES)
         for half in range(HALVES):
             nc.sync.dma_start(
-                out=out_halves[half], in_=y_sb[half][:].rearrange("o (b s) -> o b s", b=2)
+                out=out_halves[half], in_=y_sb[half][:].rearrange("o (b ij) -> o b ij", b=BATCH)
             )

@@ -159,10 +159,6 @@ def tile_skconv2d_pa_s_kernel(tc, xw, S1s, U1s, U2s, S2s, bias, out):
         )
         quantise(x_grp[:], x_codes[:], x_scales[:])
 
-        bias_bank = psum_t.tile([P, P], BF16, tag="t")
-        nc.tensor.transpose(bias_bank[:], bias_rows[:], ident_bf16[:])
-        nc.scalar.mul(out=bias_twice[:], in_=bias_bank[:, 0:HALVES], mul=2.0)
-
         u2_grp_words = u2_grp[:].bitcast(F32).rearrange(
             "p (piece m u) -> p piece m u", m=P, u=WORDS
         )
@@ -174,6 +170,10 @@ def tile_skconv2d_pa_s_kernel(tc, xw, S1s, U1s, U2s, S2s, bias, out):
                 out=u2_grp_words[:, PAIR * pair : PAIR * (pair + 1)],
                 in_=bank[:].rearrange("p which u m -> p which m u"),
             )
+
+        bias_bank = psum_t.tile([P, P], BF16, tag="t")
+        nc.tensor.transpose(bias_bank[:], bias_rows[:], ident_bf16[:])
+        nc.scalar.mul(out=bias_twice[:], in_=bias_bank[:, 0:HALVES], mul=2.0)
 
         def quantise_u2(pair):
             quantise(

@@ -148,7 +148,8 @@ def tile_skconv2d_pa_s_kernel(tc, xw, S1s, U1s, U2s, S2s, bias, out):
         for g in range(RUNS2):
             nc.sync.dma_start(out=s2_raw[:, cols(g, PACK * O)], in_=s2_rows[g])
         nc.sync.dma_start(
-            out=u1_raw[:], in_=U1s.flatten_outer_dims().rearrange("(m c) o -> m (c o)", c=PACK)
+            out=u1_raw[:].rearrange("m (c o) -> m c o", c=PACK),
+            in_=U1s.flatten_outer_dims().rearrange("(c m) o -> m c o", c=PACK),
         )
 
         x_bank = psum_t.tile([P, WORDS, P], F32, tag="t")
@@ -185,11 +186,11 @@ def tile_skconv2d_pa_s_kernel(tc, xw, S1s, U1s, U2s, S2s, bias, out):
         def regroup_s1(part):
             four = cols(part, HALF_TERMS)
             nc.vector.tensor_copy(
-                out=s1_grp[:].rearrange("p (c t q a) -> p c t q a", c=PACK, t=TERMS, a=PACK)[
-                    :, :, four
+                out=s1_grp[:].rearrange("p (t rg v a) -> p t rg a v", t=TERMS, v=GROUP, a=PACK)[
+                    :, four
                 ],
-                in_=s1_raw[:].rearrange("p (t a q c) -> p c t q a", t=TERMS, a=PACK, c=PACK)[
-                    :, :, four
+                in_=s1_raw[:].rearrange("p (t a rg v) -> p t rg a v", t=TERMS, a=PACK, v=GROUP)[
+                    :, four
                 ],
             )
 

@@ -28,6 +28,9 @@ PAIRS = K2 // P // PAIR
 GROUP = 4
 VECTOR_QUARTERS = 3
 
+BUSY_BEFORE_LOADS = 4
+BUSY_BEFORE_STAGE1 = 2
+
 FLOPS = 2 * P * (D * K1 + D * K2 + K1 * O + K2 * O)
 
 
@@ -129,6 +132,15 @@ def tile_skconv2d_pa_s_kernel(tc, xw, S1s, U1s, U2s, S2s, bias, out):
         make_identity(nc, ident_f32[:])
         make_identity(nc, ident_bf16[:])
         nc.vector.memset(bias_rows[:], 0.0)
+        zeros = sbuf.tile([P, P], F32)
+        nc.vector.memset(zeros[:], 0.0)
+        warm_bank = psum_y.tile([P, P], F32, tag="y")
+
+        def keep_busy(times):
+            for i in range(times):
+                nc.tensor.matmul(warm_bank[:], lhsT=zeros[:], rhs=zeros[:], start=True, stop=True)
+
+        keep_busy(BUSY_BEFORE_LOADS)
         nc.scalar.dma_start(
             out=bias_rows[0:HALVES, :], in_=bias.rearrange("(half o) -> half o", half=HALVES)
         )
@@ -206,6 +218,7 @@ def tile_skconv2d_pa_s_kernel(tc, xw, S1s, U1s, U2s, S2s, bias, out):
             psum_h.tile([P, PACK, P], F32, tag="h", name="h2_bank%d" % g) for g in range(RUNS2)
         ]
         h1_bank = psum_h.tile([P, PACK, P], F32, tag="h")
+        keep_busy(BUSY_BEFORE_STAGE1)
         stage1(h2_banks[0], u2_codes, u2_scales, 0)
         stage1(h1_bank, s1_codes, s1_scales, 0)
         stage1(h2_banks[1], u2_codes, u2_scales, PACK)

@@ -26,7 +26,7 @@ WORDS = 2
 PAIR = 2
 PAIRS = K2 // P // PAIR
 GROUP = 4
-VECTOR_QUARTERS = 3
+VECTOR_QUARTERS = 2
 
 BUSY_BEFORE_LOADS = 4
 BUSY_BEFORE_STAGE1 = 2
@@ -48,8 +48,7 @@ def tile_skconv2d_pa_s_kernel(tc, xw, S1s, U1s, U2s, S2s, bias, out):
         ctx.enter_context(tc.manual_schedule())
 
         ident_f32 = sbuf.tile([P, P], F32)
-        ident_bf16 = sbuf.tile([P, P], BF16)
-        bias_rows = sbuf.tile([P, P], BF16)
+        bias_rows = sbuf.tile([P, O], BF16)
         bias_twice = sbuf.tile([P, HALVES], F32)
 
         x_raw = sbuf.tile([P, D], BF16)
@@ -81,7 +80,7 @@ def tile_skconv2d_pa_s_kernel(tc, xw, S1s, U1s, U2s, S2s, bias, out):
         h2_codes = sbuf.tile([P, RUNS2 * P], U32, align_bytes=64)
         h2_scales = sbuf.tile([P, RUNS2 * P], U8, align_bytes=64)
 
-        y_sb = [sbuf.tile([P, P], F32, name="y_sb%d" % half) for half in range(HALVES)]
+        y_sb = sbuf.tile([P, BATCH, HALVES, P // BATCH], F32)
 
         def quantise(grouped, codes, scales):
             nc.vector.quantize_mx(out=codes.bitcast(FP8X4), scales=scales, in_=grouped)
@@ -92,11 +91,11 @@ def tile_skconv2d_pa_s_kernel(tc, xw, S1s, U1s, U2s, S2s, bias, out):
                 nc.tensor.transpose(bank[:, u, :], words[:, u, :], ident_f32[:])
 
         def regroup_rows(grouped, rows, width):
-            to = grouped.rearrange("m (wg v c) -> m wg c v", v=GROUP, c=PACK)
-            frm = rows.rearrange("m (c wg v) -> m wg c v", v=GROUP, c=PACK)
-            cut = (width // GROUP) * VECTOR_QUARTERS // 4
-            nc.vector.tensor_copy(out=to[:, 0:cut], in_=frm[:, 0:cut])
-            nc.scalar.copy(out=to[:, cut:], in_=frm[:, cut:])
+            to = grouped.rearrange("m (half og v c) -> m half og c v", half=HALVES, v=GROUP, c=PACK)
+            frm = rows.rearrange("m (c og v half) -> m half og c v", half=HALVES, v=GROUP, c=PACK)
+            cut = (width // HALVES // GROUP) * VECTOR_QUARTERS // 4
+            nc.vector.tensor_copy(out=to[:, :, 0:cut], in_=frm[:, :, 0:cut])
+            nc.scalar.copy(out=to[:, :, cut:], in_=frm[:, :, cut:])
 
         def stage1(h_bank, w_codes, w_scales, first_piece):
             for c in range(PACK):
@@ -130,7 +129,6 @@ def tile_skconv2d_pa_s_kernel(tc, xw, S1s, U1s, U2s, S2s, bias, out):
                 )
 
         make_identity(nc, ident_f32[:])
-        make_identity(nc, ident_bf16[:])
         nc.vector.memset(bias_rows[:], 0.0)
         zeros = sbuf.tile([P, P], F32)
         nc.vector.memset(zeros[:], 0.0)
@@ -142,7 +140,7 @@ def tile_skconv2d_pa_s_kernel(tc, xw, S1s, U1s, U2s, S2s, bias, out):
 
         keep_busy(BUSY_BEFORE_LOADS)
         nc.scalar.dma_start(
-            out=bias_rows[0:HALVES, :], in_=bias.rearrange("(half o) -> half o", half=HALVES)
+            out=bias_rows[0:1, :], in_=bias.rearrange("(one o) -> one o", one=1)
         )
 
         u2_rows = U2s.flatten_outer_dims().rearrange("(g m c) d -> m g c d", g=RUNS2, c=PACK)
@@ -184,9 +182,9 @@ def tile_skconv2d_pa_s_kernel(tc, xw, S1s, U1s, U2s, S2s, bias, out):
                 in_=bank[:].rearrange("p which u m -> p which m u"),
             )
 
-        bias_bank = psum_t.tile([P, P], BF16, tag="t")
-        nc.tensor.transpose(bias_bank[:], bias_rows[:], ident_bf16[:])
-        nc.scalar.mul(out=bias_twice[:], in_=bias_bank[:, 0:HALVES], mul=2.0)
+        bias_bank = psum_t.tile([P, P], F32, tag="t")
+        nc.tensor.transpose(bias_bank[:], bias_rows[:].bitcast(F32), ident_f32[:])
+        nc.scalar.mul(out=bias_twice[:], in_=bias_bank[:].bitcast(BF16)[:, 0:HALVES], mul=2.0)
 
         def quantise_u2(pair):
             quantise(
@@ -259,22 +257,21 @@ def tile_skconv2d_pa_s_kernel(tc, xw, S1s, U1s, U2s, S2s, bias, out):
         stage2_of_h2(1, start=False, stop=True)
 
         nc.scalar.activation(
-            out=y_sb[0][:],
-            in_=y_banks[0][:],
+            out=y_sb[:, :, 0, :],
+            in_=y_banks[0][:].rearrange("o (b ij) -> o b ij", b=BATCH),
             func=mybir.ActivationFunctionType.Identity,
             bias=bias_twice[:, 0:1],
             scale=1.0 / TERMS,
         )
         nc.vector.tensor_scalar(
-            out=y_sb[1][:],
-            in0=y_banks[1][:],
+            out=y_sb[:, :, 1, :],
+            in0=y_banks[1][:].rearrange("o (b ij) -> o b ij", b=BATCH),
             scalar1=1.0 / TERMS,
             scalar2=bias_twice[:, 1:2],
             op0=mybir.AluOpType.mult,
             op1=mybir.AluOpType.add,
         )
-        out_halves = out.rearrange("b (half o) i j -> half o b (i j)", half=HALVES)
-        for half in range(HALVES):
-            nc.sync.dma_start(
-                out=out_halves[half], in_=y_sb[half][:].rearrange("o (b ij) -> o b ij", b=BATCH)
-            )
+        nc.sync.dma_start(
+            out=out.rearrange("b (o half) i j -> o b (half i j)", half=HALVES),
+            in_=y_sb[:].rearrange("o b half ij -> o b (half ij)"),
+        )

@@ -28,8 +28,9 @@ PAIRS = K2 // P // PAIR
 GROUP = 4
 VECTOR_QUARTERS = 2
 
-BUSY_BEFORE_LOADS = 4
+BUSY_BEFORE_LOADS = 3
 BUSY_BEFORE_STAGE1 = 2
+BUSY_BEFORE_STAGE2 = 2
 
 FLOPS = 2 * P * (D * K1 + D * K2 + K1 * O + K2 * O)
 
@@ -90,12 +91,38 @@ def tile_skconv2d_pa_s_kernel(tc, xw, S1s, U1s, U2s, S2s, bias, out):
             for u in range(WORDS):
                 nc.tensor.transpose(bank[:, u, :], words[:, u, :], ident_f32[:])
 
-        def regroup_rows(grouped, rows, width):
-            to = grouped.rearrange("m (half og v c) -> m half og c v", half=HALVES, v=GROUP, c=PACK)
-            frm = rows.rearrange("m (c og v half) -> m half og c v", half=HALVES, v=GROUP, c=PACK)
-            cut = (width // HALVES // GROUP) * VECTOR_QUARTERS // 4
-            nc.vector.tensor_copy(out=to[:, :, 0:cut], in_=frm[:, :, 0:cut])
-            nc.scalar.copy(out=to[:, :, cut:], in_=frm[:, :, cut:])
+        def share(vector_part, to, frm, axis):
+            at = lambda part: tuple([slice(None)] * axis + [part])
+            count = to.shape[axis]
+            if vector_part > 0:
+                nc.vector.tensor_copy(out=to[at(slice(0, vector_part))], in_=frm[at(slice(0, vector_part))])
+            if vector_part < count:
+                nc.scalar.copy(
+                    out=to[at(slice(vector_part, count))], in_=frm[at(slice(vector_part, count))]
+                )
+
+        def regroup_rows(grouped, rows, vector_groups):
+            share(
+                vector_groups,
+                grouped.rearrange("m (half og v c) -> m og c v half", half=HALVES, v=GROUP // HALVES, c=PACK),
+                rows.rearrange("m (c og v half) -> m og c v half", half=HALVES, v=GROUP // HALVES, c=PACK),
+                1,
+            )
+
+        def regroup_s2(g, vector_groups):
+            regroup_rows(s2_grp[:, cols(g, O * PACK)], s2_raw[:, cols(g, O * PACK)], vector_groups)
+
+        def regroup_u1(vector_groups):
+            regroup_rows(u1_grp[:], u1_raw[:], vector_groups)
+
+        def regroup_s1(part, vector_terms):
+            four = cols(part, HALF_TERMS)
+            share(
+                vector_terms,
+                s1_grp[:].rearrange("p (t rg v a) -> p t rg a v", t=TERMS, v=GROUP, a=PACK)[:, four],
+                s1_raw[:].rearrange("p (t a rg v) -> p t rg a v", t=TERMS, a=PACK, v=GROUP)[:, four],
+                1,
+            )
 
         def stage1(h_bank, w_codes, w_scales, first_piece):
             for c in range(PACK):
@@ -148,43 +175,69 @@ def tile_skconv2d_pa_s_kernel(tc, xw, S1s, U1s, U2s, S2s, bias, out):
         s1_rows = S1s.rearrange("t (p a) r -> p t (a r)", a=PACK)
         s1_raw_terms = s1_raw[:].rearrange("p (t ar) -> p t ar", t=TERMS)
         s2_rows = S2s.flatten_outer_dims().rearrange("(g m c) o -> g m (c o)", g=RUNS2, c=PACK)
-        nc.sync.dma_start(out=x_raw[:], in_=xw)
-        for g in range(RUNS2):
-            for first_c in range(0, PACK, PAIR):
-                two = slice(first_c, first_c + PAIR)
-                nc.sync.dma_start(out=u2_raw_pieces[:, g, two, :], in_=u2_rows[:, g, two, :])
-            four = cols(g, HALF_TERMS)
-            nc.sync.dma_start(out=s1_raw_terms[:, four, :], in_=s1_rows[:, four, :])
-        for g in range(RUNS2):
-            nc.sync.dma_start(out=s2_raw[:, cols(g, PACK * O)], in_=s2_rows[g])
-        nc.sync.dma_start(
-            out=u1_raw[:].rearrange("m (c o) -> m c o", c=PACK),
-            in_=U1s.flatten_outer_dims().rearrange("(c m) o -> m c o", c=PACK),
-        )
+        def load_x():
+            nc.sync.dma_start(out=x_raw[:], in_=xw)
 
-        x_bank = psum_t.tile([P, WORDS, P], F32, tag="t")
-        transpose_rows(x_bank, x_raw[:])
-        nc.scalar.copy(
-            out=x_grp[:].bitcast(F32).rearrange("p (n u) -> p n u", u=WORDS),
-            in_=x_bank[:].rearrange("p u n -> p n u"),
-        )
-        quantise(x_grp[:], x_codes[:], x_scales[:])
+        def load_u2(pair):
+            g, half = divmod(pair, PACK // PAIR)
+            two = cols(half, PAIR)
+            nc.sync.dma_start(out=u2_raw_pieces[:, g, two, :], in_=u2_rows[:, g, two, :])
+
+        def load_s1(part):
+            four = cols(part, HALF_TERMS)
+            nc.sync.dma_start(out=s1_raw_terms[:, four, :], in_=s1_rows[:, four, :])
+
+        def load_s2(g):
+            nc.sync.dma_start(out=s2_raw[:, cols(g, PACK * O)], in_=s2_rows[g])
+
+        def load_u1():
+            nc.sync.dma_start(
+                out=u1_raw[:].rearrange("m (c o) -> m c o", c=PACK),
+                in_=U1s.flatten_outer_dims().rearrange("(c m) o -> m c o", c=PACK),
+            )
+
+        load_x()
+        load_u2(0)
+        load_u2(1)
+        load_s1(0)
+        load_u2(2)
+        load_u2(3)
+        load_s1(1)
+        load_s2(0)
+        load_s2(1)
+        load_u1()
+
+        def transpose_x(copy):
+            bank = psum_t.tile([P, WORDS, P], F32, tag="t", name="x_bank")
+            transpose_rows(bank, x_raw[:])
+            copy(
+                out=x_grp[:].bitcast(F32).rearrange("p (n u) -> p n u", u=WORDS),
+                in_=bank[:].rearrange("p u n -> p n u"),
+            )
 
         u2_grp_words = u2_grp[:].bitcast(F32).rearrange(
             "p (piece m u) -> p piece m u", m=P, u=WORDS
         )
-        for pair in range(PAIRS):
-            bank = psum_t.tile([P, PAIR, WORDS, P], F32, tag="t")
+
+        def transpose_u2(pair, copy):
+            bank = psum_t.tile([P, PAIR, WORDS, P], F32, tag="t", name="u2_bank")
             for which in range(PAIR):
                 transpose_rows(bank[:, which], u2_raw[:, cols(PAIR * pair + which, D)])
-            nc.scalar.copy(
+            copy(
                 out=u2_grp_words[:, PAIR * pair : PAIR * (pair + 1)],
                 in_=bank[:].rearrange("p which u m -> p which m u"),
             )
 
-        bias_bank = psum_t.tile([P, P], F32, tag="t")
-        nc.tensor.transpose(bias_bank[:], bias_rows[:].bitcast(F32), ident_f32[:])
-        nc.scalar.mul(out=bias_twice[:], in_=bias_bank[:].bitcast(BF16)[:, 0:HALVES], mul=2.0)
+        def transpose_bias():
+            bank = psum_t.tile([P, P], F32, tag="t", name="bias_bank")
+            nc.tensor.transpose(bank[:], bias_rows[:].bitcast(F32), ident_f32[:])
+            return bank
+
+        def double_bias(bank):
+            nc.scalar.mul(out=bias_twice[:], in_=bank[:].bitcast(BF16)[:, 0:HALVES], mul=2.0)
+
+        def quantise_x():
+            quantise(x_grp[:], x_codes[:], x_scales[:])
 
         def quantise_u2(pair):
             quantise(
@@ -193,51 +246,76 @@ def tile_skconv2d_pa_s_kernel(tc, xw, S1s, U1s, U2s, S2s, bias, out):
                 u2_scales[:, cols(pair, PAIR * P)],
             )
 
-        def regroup_s1(part):
-            four = cols(part, HALF_TERMS)
-            nc.vector.tensor_copy(
-                out=s1_grp[:].rearrange("p (t rg v a) -> p t rg a v", t=TERMS, v=GROUP, a=PACK)[
-                    :, four
-                ],
-                in_=s1_raw[:].rearrange("p (t a rg v) -> p t rg a v", t=TERMS, a=PACK, v=GROUP)[
-                    :, four
-                ],
-            )
+        def quantise_s1():
+            quantise(s1_grp[:], s1_codes[:], s1_scales[:])
 
-        regroup_s1(0)
-        quantise_u2(0)
-        regroup_s1(1)
-        quantise_u2(1)
-        quantise_u2(2)
-        quantise(s1_grp[:], s1_codes[:], s1_scales[:])
-        quantise_u2(3)
+        def quantise_s2():
+            quantise(s2_grp[:], s2_codes[:], s2_scales[:])
+
+        def quantise_u1():
+            quantise(u1_grp[:], u1_codes[:], u1_scales[:])
+
+        def quantise_h1():
+            quantise(h1_grp[:], h1_codes[:], h1_scales[:])
+
+        def quantise_h2(g):
+            quantise(h2_grp[:, cols(g, P * PACK)], h2_codes[:, cols(g, P)], h2_scales[:, cols(g, P)])
 
         h2_banks = [
             psum_h.tile([P, PACK, P], F32, tag="h", name="h2_bank%d" % g) for g in range(RUNS2)
         ]
         h1_bank = psum_h.tile([P, PACK, P], F32, tag="h")
+
+        def stage1_h1():
+            stage1(h1_bank, s1_codes, s1_scales, 0)
+
+        def stage1_h2(g):
+            stage1(h2_banks[g], u2_codes, u2_scales, g * PACK)
+
+        def round_h1():
+            round_h(h1_bank, h1_grp[:])
+
+        def round_h2(g):
+            round_h(h2_banks[g], h2_grp[:, cols(g, P * PACK)])
+
+        on_scalar, on_vector = nc.scalar.copy, nc.vector.tensor_copy
+
+        transpose_x(on_scalar)
+        transpose_u2(0, on_scalar)
+        transpose_u2(1, on_scalar)
+        transpose_u2(2, on_scalar)
+        transpose_u2(3, on_scalar)
+        bias_bank = transpose_bias()
+        quantise_x()
+        regroup_s1(0, 4)
+        quantise_u2(0)
+        regroup_s1(1, 4)
+        quantise_u2(1)
+        quantise_u2(2)
+        quantise_s1()
+        quantise_u2(3)
         keep_busy(BUSY_BEFORE_STAGE1)
-        stage1(h2_banks[0], u2_codes, u2_scales, 0)
-        stage1(h1_bank, s1_codes, s1_scales, 0)
-        stage1(h2_banks[1], u2_codes, u2_scales, PACK)
-
-        for g in range(RUNS2):
-            regroup_rows(s2_grp[:, cols(g, O * PACK)], s2_raw[:, cols(g, O * PACK)], O)
-        regroup_rows(u1_grp[:], u1_raw[:], O)
-
-        def quantise_h2(g):
-            quantise(h2_grp[:, cols(g, P * PACK)], h2_codes[:, cols(g, P)], h2_scales[:, cols(g, P)])
-
-        round_h(h2_banks[0], h2_grp[:, cols(0, P * PACK)])
-        round_h(h1_bank, h1_grp[:])
-        round_h(h2_banks[1], h2_grp[:, cols(1, P * PACK)])
-
-        quantise(s2_grp[:], s2_codes[:], s2_scales[:])
+        stage1_h2(0)
+        stage1_h1()
+        stage1_h2(1)
+        keep_busy(BUSY_BEFORE_STAGE2)
+        regroup_s2(0, 32)
+        regroup_s2(1, 32)
+        regroup_u1(48)
+        round_h2(0)
+        round_h1()
+        round_h2(1)
+        double_bias(bias_bank)
+        quantise_s2()
         quantise_h2(0)
-        quantise(u1_grp[:], u1_codes[:], u1_scales[:])
-        quantise(h1_grp[:], h1_codes[:], h1_scales[:])
+        quantise_u1()
+        quantise_h1()
         quantise_h2(1)
 
+        h2_banks = [
+            psum_h.tile([P, PACK, P], F32, tag="h", name="h2_bank%d" % g) for g in range(RUNS2)
+        ]
+        h1_bank = psum_h.tile([P, PACK, P], F32, tag="h")
         y_banks = [
             psum_y.tile([P, P], F32, tag="y", name="y_bank%d" % half) for half in range(HALVES)
         ]

@@ -156,7 +156,6 @@ def tile_skconv2d_pa_s_kernel(tc, xw, S1s, U1s, U2s, S2s, bias, out):
                 )
 
         make_identity(nc, ident_f32[:])
-        nc.vector.memset(bias_rows[:], 0.0)
         zeros = sbuf.tile([P, P], F32)
         nc.vector.memset(zeros[:], 0.0)
         warm_bank = psum_y.tile([P, P], F32, tag="y")
@@ -166,9 +165,7 @@ def tile_skconv2d_pa_s_kernel(tc, xw, S1s, U1s, U2s, S2s, bias, out):
                 nc.tensor.matmul(warm_bank[:], lhsT=zeros[:], rhs=zeros[:], start=True, stop=True)
 
         keep_busy(BUSY_BEFORE_LOADS)
-        nc.scalar.dma_start(
-            out=bias_rows[0:1, :], in_=bias.rearrange("(one o) -> one o", one=1)
-        )
+        nc.vector.memset(bias_rows[:], 0.0)
 
         u2_rows = U2s.flatten_outer_dims().rearrange("(g m c) d -> m g c d", g=RUNS2, c=PACK)
         u2_raw_pieces = u2_raw[:].rearrange("m (g c d) -> m g c d", g=RUNS2, c=PACK)
@@ -206,6 +203,7 @@ def tile_skconv2d_pa_s_kernel(tc, xw, S1s, U1s, U2s, S2s, bias, out):
         load_s2(0)
         load_s2(1)
         load_u1()
+        nc.sync.dma_start(out=bias_rows[0:1, :], in_=bias.rearrange("(one o) -> one o", one=1))
 
         def transpose_x(copy):
             bank = psum_t.tile([P, WORDS, P], F32, tag="t", name="x_bank")
@@ -285,12 +283,11 @@ def tile_skconv2d_pa_s_kernel(tc, xw, S1s, U1s, U2s, S2s, bias, out):
         transpose_u2(1, on_scalar)
         transpose_u2(2, on_scalar)
         transpose_u2(3, on_scalar)
-        bias_bank = transpose_bias()
         quantise_x()
         regroup_s1(0, 4)
         quantise_u2(0)
-        regroup_s1(1, 4)
         quantise_u2(1)
+        regroup_s1(1, 4)
         quantise_u2(2)
         quantise_s1()
         quantise_u2(3)
@@ -299,8 +296,9 @@ def tile_skconv2d_pa_s_kernel(tc, xw, S1s, U1s, U2s, S2s, bias, out):
         stage1_h1()
         stage1_h2(1)
         keep_busy(BUSY_BEFORE_STAGE2)
-        regroup_s2(0, 32)
-        regroup_s2(1, 32)
+        bias_bank = transpose_bias()
+        regroup_s2(0, 0)
+        regroup_s2(1, 64)
         regroup_u1(48)
         round_h2(0)
         round_h1()
@@ -312,10 +310,6 @@ def tile_skconv2d_pa_s_kernel(tc, xw, S1s, U1s, U2s, S2s, bias, out):
         quantise_h1()
         quantise_h2(1)
 
-        h2_banks = [
-            psum_h.tile([P, PACK, P], F32, tag="h", name="h2_bank%d" % g) for g in range(RUNS2)
-        ]
-        h1_bank = psum_h.tile([P, PACK, P], F32, tag="h")
         y_banks = [
             psum_y.tile([P, P], F32, tag="y", name="y_bank%d" % half) for half in range(HALVES)
         ]

from contextlib import ExitStack

import concourse.mybir as mybir
from concourse.masks import make_identity

F32 = mybir.dt.float32
BF16 = mybir.dt.bfloat16
U32 = mybir.dt.uint32
U8 = mybir.dt.uint8
FP8X4 = mybir.dt.float8_e4m3fn_x4

P = 128
PACK = 4
RUN = P * PACK
D = 512
K1 = 512
K2 = 1024
RUNS2 = K2 // RUN
TERMS = 8
HALF_TERMS = TERMS // 2
RANK1 = 64
O = 256
HALVES = O // P
BATCH = 2
WORDS = 2
PAIR = 2
PAIRS = K2 // P // PAIR
GROUP = 4
VECTOR_QUARTERS = 2

BUSY_BEFORE_LOADS = 3
BUSY_BEFORE_STAGE1 = 2
BUSY_BEFORE_STAGE2 = 2

FLOPS = 2 * P * (D * K1 + D * K2 + K1 * O + K2 * O)


def cols(index, width):
    return slice(index * width, (index + 1) * width)


def tile_skconv2d_pa_s_kernel(tc, xw, S1s, U1s, U2s, S2s, bias, out):
    nc = tc.nc
    with ExitStack() as ctx:
        sbuf = ctx.enter_context(tc.tile_pool(name="sbuf", bufs=1))
        psum_t = ctx.enter_context(tc.psum_pool(name="psum_t", bufs=3))
        psum_h = ctx.enter_context(tc.psum_pool(name="psum_h", bufs=RUNS2 + 1))
        psum_y = ctx.enter_context(tc.psum_pool(name="psum_y", bufs=HALVES))
        ctx.enter_context(tc.manual_schedule())

        ident_f32 = sbuf.tile([P, P], F32)
        bias_rows = sbuf.tile([P, O], BF16)
        bias_twice = sbuf.tile([P, HALVES], F32)

        x_raw = sbuf.tile([P, D], BF16)
        u2_raw = sbuf.tile([P, RUNS2 * PACK * D], BF16)
        s1_raw = sbuf.tile([P, TERMS * PACK * RANK1], BF16)
        s2_raw = sbuf.tile([P, RUNS2 * PACK * O], BF16)
        u1_raw = sbuf.tile([P, PACK * O], BF16)

        x_grp = sbuf.tile([P, P * PACK], BF16, align_bytes=64)
        u2_grp = sbuf.tile([P, K2 * PACK], BF16, align_bytes=64)
        s1_grp = sbuf.tile([P, K1 * PACK], BF16, align_bytes=64)
        s2_grp = sbuf.tile([P, RUNS2 * O * PACK], BF16, align_bytes=64)
        u1_grp = sbuf.tile([P, O * PACK], BF16, align_bytes=64)
        h1_grp = sbuf.tile([P, P * PACK], BF16, align_bytes=64)
        h2_grp = sbuf.tile([P, RUNS2 * P * PACK], BF16, align_bytes=64)

        x_codes = sbuf.tile([P, P], U32, align_bytes=64)
        x_scales = sbuf.tile([P, P], U8, align_bytes=64)
        u2_codes = sbuf.tile([P, K2], U32, align_bytes=64)
        u2_scales = sbuf.tile([P, K2], U8, align_bytes=64)
        s1_codes = sbuf.tile([P, K1], U32, align_bytes=64)
        s1_scales = sbuf.tile([P, K1], U8, align_bytes=64)
        s2_codes = sbuf.tile([P, RUNS2 * O], U32, align_bytes=64)
        s2_scales = sbuf.tile([P, RUNS2 * O], U8, align_bytes=64)
        u1_codes = sbuf.tile([P, O], U32, align_bytes=64)
        u1_scales = sbuf.tile([P, O], U8, align_bytes=64)
        h1_codes = sbuf.tile([P, P], U32, align_bytes=64)
        h1_scales = sbuf.tile([P, P], U8, align_bytes=64)
        h2_codes = sbuf.tile([P, RUNS2 * P], U32, align_bytes=64)
        h2_scales = sbuf.tile([P, RUNS2 * P], U8, align_bytes=64)

        y_sb = sbuf.tile([P, BATCH, HALVES, P // BATCH], F32)

        def quantise(grouped, codes, scales):
            nc.vector.quantize_mx(out=codes.bitcast(FP8X4), scales=scales, in_=grouped)

        def transpose_rows(bank, rows):
            words = rows.bitcast(F32).rearrange("row (p u) -> row u p", u=WORDS)
            for u in range(WORDS):
                nc.tensor.transpose(bank[:, u, :], words[:, u, :], ident_f32[:])

        def share(vector_part, to, frm, axis):
            at = lambda part: tuple([slice(None)] * axis + [part])
            count = to.shape[axis]
            if vector_part > 0:
                nc.vector.tensor_copy(out=to[at(slice(0, vector_part))], in_=frm[at(slice(0, vector_part))])
            if vector_part < count:
                nc.scalar.copy(
                    out=to[at(slice(vector_part, count))], in_=frm[at(slice(vector_part, count))]
                )

        def regroup_rows(grouped, rows, vector_groups):
            share(
                vector_groups,
                grouped.rearrange("m (half og v c) -> m og c v half", half=HALVES, v=GROUP // HALVES, c=PACK),
                rows.rearrange("m (c og v half) -> m og c v half", half=HALVES, v=GROUP // HALVES, c=PACK),
                1,
            )

        def regroup_s2(g, vector_groups):
            regroup_rows(s2_grp[:, cols(g, O * PACK)], s2_raw[:, cols(g, O * PACK)], vector_groups)

        def regroup_u1(vector_groups):
            regroup_rows(u1_grp[:], u1_raw[:], vector_groups)

        def regroup_s1(part, vector_terms):
            four = cols(part, HALF_TERMS)
            share(
                vector_terms,
                s1_grp[:].rearrange("p (t rg v a) -> p t rg a v", t=TERMS, v=GROUP, a=PACK)[:, four],
                s1_raw[:].rearrange("p (t a rg v) -> p t rg a v", t=TERMS, a=PACK, v=GROUP)[:, four],
                1,
            )

        def stage1(h_bank, w_codes, w_scales, first_piece):
            for c in range(PACK):
                piece = cols(first_piece + c, P)
                nc.tensor.matmul_mx(
                    out=h_bank[:, c, :],
                    lhsT=w_codes[:, piece].bitcast(FP8X4),
                    lhsT_scale=w_scales[:, piece],
                    rhs=x_codes[:].bitcast(FP8X4),
                    rhs_scale=x_scales[:],
                    start=True,
                    stop=True,
                )

        def round_h(h_bank, h_grp):
            nc.scalar.copy(
                out=h_grp.rearrange("m (n c) -> m n c", c=PACK),
                in_=h_bank[:].rearrange("m c n -> m n c"),
            )

        def stage2(w_codes, w_scales, h_codes, h_scales, start, stop):
            for half in range(HALVES):
                nc.tensor.matmul_mx(
                    out=y_banks[half][:],
                    lhsT=w_codes[:, cols(half, P)].bitcast(FP8X4),
                    lhsT_scale=w_scales[:, cols(half, P)],
                    rhs=h_codes.bitcast(FP8X4),
                    rhs_scale=h_scales,
                    start=start,
                    stop=stop,
                )

        make_identity(nc, ident_f32[:])
        zeros = sbuf.tile([P, P], F32)
        nc.vector.memset(zeros[:], 0.0)
        warm_bank = psum_y.tile([P, P], F32, tag="y")

        def keep_busy(times):
            for i in range(times):
                nc.tensor.matmul(warm_bank[:], lhsT=zeros[:], rhs=zeros[:], start=True, stop=True)

        keep_busy(BUSY_BEFORE_LOADS)
        nc.vector.memset(bias_rows[:], 0.0)

        u2_rows = U2s.flatten_outer_dims().rearrange("(g m c) d -> m g c d", g=RUNS2, c=PACK)
        u2_raw_pieces = u2_raw[:].rearrange("m (g c d) -> m g c d", g=RUNS2, c=PACK)
        s1_rows = S1s.rearrange("t (p a) r -> p t (a r)", a=PACK)
        s1_raw_terms = s1_raw[:].rearrange("p (t ar) -> p t ar", t=TERMS)
        s2_rows = S2s.flatten_outer_dims().rearrange("(g m c) o -> g m (c o)", g=RUNS2, c=PACK)
        def load_x():
            nc.sync.dma_start(out=x_raw[:], in_=xw)

        def load_u2(pair):
            g, half = divmod(pair, PACK // PAIR)
            two = cols(half, PAIR)
            nc.sync.dma_start(out=u2_raw_pieces[:, g, two, :], in_=u2_rows[:, g, two, :])

        def load_s1(part):
            four = cols(part, HALF_TERMS)
            nc.sync.dma_start(out=s1_raw_terms[:, four, :], in_=s1_rows[:, four, :])

        def load_s2(g):
            nc.sync.dma_start(out=s2_raw[:, cols(g, PACK * O)], in_=s2_rows[g])

        def load_u1():
            nc.sync.dma_start(
                out=u1_raw[:].rearrange("m (c o) -> m c o", c=PACK),
                in_=U1s.flatten_outer_dims().rearrange("(c m) o -> m c o", c=PACK),
            )

        load_x()
        load_u2(0)
        load_u2(1)
        load_s1(0)
        load_u2(2)
        load_u2(3)
        load_s1(1)
        load_s2(0)
        load_s2(1)
        load_u1()
        nc.sync.dma_start(out=bias_rows[0:1, :], in_=bias.rearrange("(one o) -> one o", one=1))

        def transpose_x(copy):
            bank = psum_t.tile([P, WORDS, P], F32, tag="t", name="x_bank")
            transpose_rows(bank, x_raw[:])
            copy(
                out=x_grp[:].bitcast(F32).rearrange("p (n u) -> p n u", u=WORDS),
                in_=bank[:].rearrange("p u n -> p n u"),
            )

        u2_grp_words = u2_grp[:].bitcast(F32).rearrange(
            "p (piece m u) -> p piece m u", m=P, u=WORDS
        )

        def transpose_u2(pair, copy):
            bank = psum_t.tile([P, PAIR, WORDS, P], F32, tag="t", name="u2_bank")
            for which in range(PAIR):
                transpose_rows(bank[:, which], u2_raw[:, cols(PAIR * pair + which, D)])
            copy(
                out=u2_grp_words[:, PAIR * pair : PAIR * (pair + 1)],
                in_=bank[:].rearrange("p which u m -> p which m u"),
            )

        def transpose_bias():
            bank = psum_t.tile([P, P], F32, tag="t", name="bias_bank")
            nc.tensor.transpose(bank[:], bias_rows[:].bitcast(F32), ident_f32[:])
            return bank

        def double_bias(bank):
            nc.scalar.mul(out=bias_twice[:], in_=bank[:].bitcast(BF16)[:, 0:HALVES], mul=2.0)

        def quantise_x():
            quantise(x_grp[:], x_codes[:], x_scales[:])

        def quantise_u2(pair):
            quantise(
                u2_grp[:, cols(pair, PAIR * P * PACK)],
                u2_codes[:, cols(pair, PAIR * P)],
                u2_scales[:, cols(pair, PAIR * P)],
            )

        def quantise_s1():
            quantise(s1_grp[:], s1_codes[:], s1_scales[:])

        def quantise_s2():
            quantise(s2_grp[:], s2_codes[:], s2_scales[:])

        def quantise_u1():
            quantise(u1_grp[:], u1_codes[:], u1_scales[:])

        def quantise_h1():
            quantise(h1_grp[:], h1_codes[:], h1_scales[:])

        def quantise_h2(g):
            quantise(h2_grp[:, cols(g, P * PACK)], h2_codes[:, cols(g, P)], h2_scales[:, cols(g, P)])

        h2_banks = [
            psum_h.tile([P, PACK, P], F32, tag="h", name="h2_bank%d" % g) for g in range(RUNS2)
        ]
        h1_bank = psum_h.tile([P, PACK, P], F32, tag="h")

        def stage1_h1():
            stage1(h1_bank, s1_codes, s1_scales, 0)

        def stage1_h2(g):
            stage1(h2_banks[g], u2_codes, u2_scales, g * PACK)

        def round_h1():
            round_h(h1_bank, h1_grp[:])

        def round_h2(g):
            round_h(h2_banks[g], h2_grp[:, cols(g, P * PACK)])

        on_scalar, on_vector = nc.scalar.copy, nc.vector.tensor_copy

        transpose_x(on_scalar)
        transpose_u2(0, on_scalar)
        transpose_u2(1, on_scalar)
        transpose_u2(2, on_scalar)
        transpose_u2(3, on_scalar)
        quantise_x()
        regroup_s1(0, 4)
        quantise_u2(0)
        quantise_u2(1)
        regroup_s1(1, 4)
        quantise_u2(2)
        quantise_s1()
        quantise_u2(3)
        keep_busy(BUSY_BEFORE_STAGE1)
        stage1_h2(0)
        stage1_h1()
        stage1_h2(1)
        keep_busy(BUSY_BEFORE_STAGE2)
        bias_bank = transpose_bias()
        regroup_s2(0, 0)
        regroup_s2(1, 64)
        regroup_u1(48)
        round_h2(0)
        round_h1()
        round_h2(1)
        double_bias(bias_bank)
        quantise_s2()
        quantise_h2(0)
        quantise_u1()
        quantise_h1()
        quantise_h2(1)

        y_banks = [
            psum_y.tile([P, P], F32, tag="y", name="y_bank%d" % half) for half in range(HALVES)
        ]

        def stage2_of_h2(g, start, stop):
            stage2(
                s2_codes[:, cols(g, O)],
                s2_scales[:, cols(g, O)],
                h2_codes[:, cols(g, P)],
                h2_scales[:, cols(g, P)],
                start=start,
                stop=stop,
            )

        stage2_of_h2(0, start=True, stop=False)
        stage2(u1_codes[:], u1_scales[:], h1_codes[:], h1_scales[:], start=False, stop=False)
        stage2_of_h2(1, start=False, stop=True)

        nc.scalar.activation(
            out=y_sb[:, :, 0, :],
            in_=y_banks[0][:].rearrange("o (b ij) -> o b ij", b=BATCH),
            func=mybir.ActivationFunctionType.Identity,
            bias=bias_twice[:, 0:1],
            scale=1.0 / TERMS,
        )
        nc.vector.tensor_scalar(
            out=y_sb[:, :, 1, :],
            in0=y_banks[1][:].rearrange("o (b ij) -> o b ij", b=BATCH),
            scalar1=1.0 / TERMS,
            scalar2=bias_twice[:, 1:2],
            op0=mybir.AluOpType.mult,
            op1=mybir.AluOpType.add,
        )
        nc.sync.dma_start(
            out=out.rearrange("b (o half) i j -> o b (half i j)", half=HALVES),
            in_=y_sb[:].rearrange("o b half ij -> o b (half ij)"),
        )
